import numpy as np
import ml_dtypes


def mxq(x, axis, fmt="e4m3"):
    dtype, down = {"e4m3": (ml_dtypes.float8_e4m3fn, 7), "e5m2": (ml_dtypes.float8_e5m2, 14)}[fmt]
    v = np.moveaxis(np.asarray(x, np.float32).astype(ml_dtypes.bfloat16).astype(np.float64), axis, -1)
    blocks = v.reshape(v.shape[:-1] + (-1, 32))
    amax = np.abs(blocks).max(-1, keepdims=True)
    byte = np.maximum(np.where(amax > 0, np.frexp(amax)[1] - 1 + 127, 0) - down, 1)
    scale = np.exp2(byte - 127.0)
    codes = (blocks / scale).astype(np.float32).astype(dtype).astype(np.float64)
    return np.moveaxis((codes * scale).reshape(v.shape), -1, axis)


WIDE = False


def mx_kscale(k):
    if not WIDE:
        return np.ones(k)
    levels = np.array([10, -10, 5, -5, 0])
    if k % 512:
        return np.exp2(np.random.permutation(np.resize(levels, k // 32))).repeat(32)
    a = np.empty((k // 512, 16))
    for p in range(k // 512):
        a[p, :8] = np.random.permutation(np.resize(levels, 8))
        for g in range(8):
            far = levels[np.abs(levels - a[p, g]) >= 10]
            a[p, g + 8] = far[np.random.randint(len(far))]
    return np.exp2(a.ravel()).repeat(32)


BF16 = ml_dtypes.bfloat16


def bf(x):
    return np.asarray(x, np.float32).astype(BF16)


def f64(x):
    return np.asarray(x).astype(np.float64)


B, H, D, DV, N = 1, 4, 512, 512, 1024
DIM = H * DV


def draw0():
    s, t = mx_kscale(N), mx_kscale(D)
    c = np.exp2(np.round(np.log2(s.mean())))
    q = (np.random.standard_normal((B, H, D, N)) - 1.0) * 3.0 / np.sqrt(D) / t[:, None]
    k = (np.random.standard_normal((B, H, D, N)) - 1.0) * 3.0 / np.sqrt(N) * t[:, None] * s
    v = np.random.standard_normal((B, H, DV, N)) * 0.125 * np.sqrt(N) * c / s
    return {"q": bf(q), "k": bf(k), "v": bf(v)}


def core(q, k, v):
    qr = np.maximum(f64(q), 0.0)
    kr = np.maximum(f64(k), 0.0)
    vk = mxq(f64(v), 3, "e4m3") @ mxq(kr, 3, "e4m3").transpose(0, 1, 3, 2)
    ksum = kr.sum(-1)
    num = mxq(vk, 3, "e4m3") @ mxq(qr, 2, "e4m3")
    den = (ksum[..., None] * qr).sum(-2, keepdims=True)
    out = num / den
    return out.transpose(0, 2, 1, 3).reshape(B, -1, DIM)


def e4m3fn_bytes(y):
    return np.clip(np.asarray(y, np.float64), -448.0, 448.0).astype(np.float32).astype(ml_dtypes.float8_e4m3fn).view(np.uint8)


def e4m3fn_values(b):
    return np.asarray(b, np.uint8).view(ml_dtypes.float8_e4m3fn).astype(np.float64)


def setup_inputs():
    d = draw0()
    x0 = np.asarray(d['v']).astype(np.float64)
    s = (np.max(np.abs(x0), axis=(0, 1, 2), keepdims=True) / 448.0).astype(np.float32)
    out = {}
    for k, v in d.items():
        if k == 'v':
            out['v_bytes'] = e4m3fn_bytes(x0 / s.astype(np.float64))
            out['v_scale'] = s
        else:
            out[k] = v
    return out


def reference(q, k, v_bytes, v_scale):
    return core(q, k, e4m3fn_values(v_bytes) * v_scale.astype(np.float64))

@@ -1,0 +1,247 @@
+from contextlib import ExitStack
+
+import concourse.mybir as mybir
+from concourse.masks import make_identity
+
+F32 = mybir.dt.float32
+BF16 = mybir.dt.bfloat16
+U32 = mybir.dt.uint32
+U8 = mybir.dt.uint8
+FP8 = mybir.dt.float8_e4m3fn
+FP8X4 = mybir.dt.float8_e4m3fn_x4
+ALU = mybir.AluOpType
+ACT = mybir.ActivationFunctionType
+AX = mybir.AxisListType
+
+H, D, DV, N = 4, 512, 512, 1024
+P = 128
+PACK = 4
+PASS = P * PACK
+NP = N // PASS
+FLOPS = 2 * 2 * H * D * DV * N
+
+
+def tile_relu_linear_att_pa_kernel(tc, q, k, v_bytes, v_scale, out):
+    nc = tc.nc
+    k_v = k[0].rearrange("h (m t) n -> h m t n", t=PACK)
+    v_v = v_bytes[0].rearrange("h (m s) n -> h m s n", s=PACK)
+    q_v = q[0].rearrange("h (p j) n -> h p j n", j=PACK)
+    out_v = out[0].rearrange("(m s a) (b n) -> s a b m n", s=PACK, a=2, b=2)
+    sc_v = v_scale.rearrange("a b c n -> (a b c n)")
+
+    with ExitStack() as ctx:
+        keep = ctx.enter_context(tc.tile_pool(name="keep", bufs=1))
+        ld = ctx.enter_context(tc.tile_pool(name="ld", bufs=4))
+        work = ctx.enter_context(tc.tile_pool(name="work", bufs=2))
+        psum = ctx.enter_context(tc.psum_pool(name="psum", bufs=1))
+
+        ident = keep.tile([P, P], F32, name="ident")
+        make_identity(nc, ident[:])
+        warm = keep.tile([P, 1], F32, name="warm")
+        nc.vector.memset(warm[:], 0.0)
+        nc.scalar.activation(out=warm[:], in_=warm[:], func=ACT.Relu)
+
+        scale = keep.tile([P, N], F32, name="scale")
+
+        K, V, Q, KC, KS, VC, VS, KSUM = {}, {}, {}, {}, {}, {}, {}, {}
+        QG, QC, QS, VKC, VKS, RB = {}, {}, {}, {}, {}, {}
+
+        def load_k(h):
+            t_k = ld.tile([P, PACK, N], BF16, name="t_k")
+            if h == 0:
+                for t in range(PACK):
+                    nc.sync.dma_start(out=t_k[:, t, :], in_=k_v[h][:, t, :])
+            else:
+                nc.sync.dma_start(out=t_k[:], in_=k_v[h])
+            K[h] = t_k
+
+        def load_v(h):
+            t_v = ld.tile([P, PACK, N], U8, name="t_v")
+            if h == 0:
+                for s in range(PACK):
+                    nc.sync.dma_start(out=t_v[:, s, :], in_=v_v[h][:, s, :])
+            else:
+                nc.sync.dma_start(out=t_v[:], in_=v_v[h])
+            V[h] = t_v
+
+        def load_q(h):
+            t_q = ld.tile([P, PACK, N], BF16, name="t_q")
+            nc.sync.dma_start(out=t_q[:], in_=q_v[h])
+            Q[h] = t_q
+
+        def prep_k(h):
+            kr = work.tile([P, PACK, N], BF16, name="kr", align_bytes=64)
+            ksum = work.tile([P, PACK], F32, name="ksum")
+            for t in range(PACK):
+                nc.scalar.activation(
+                    out=kr[:, t, :].rearrange("m (u x e) -> m u x e", u=2, e=2),
+                    in_=K[h][:, t, :].rearrange("m (x u e) -> m u x e", u=2, e=2),
+                    func=ACT.Relu,
+                    accum_out=ksum[:, t : t + 1],
+                )
+            KSUM[h] = ksum
+            words = kr[:].bitcast(F32)
+            codes = work.tile([P, NP, D], U32, name="kcodes", align_bytes=64)
+            scales = work.tile([P, NP, D], U8, name="kscales", align_bytes=64)
+            for g in range(NP):
+                grouped = work.tile([P, D, PACK], BF16, name="kg", align_bytes=64)
+                gw = grouped[:].rearrange("p d j -> p (d j)").bitcast(F32)
+                for half in range(2):
+                    bank = psum.tile([P, 2, 2, P], F32, name="tr", bufs=3)
+                    for r in range(2):
+                        t = 2 * half + r
+                        for u in range(2):
+                            w0 = u * 256 + g * P
+                            nc.tensor.transpose(bank[:, r, u, :], words[:, t, w0 : w0 + P], ident[:])
+                    nc.scalar.copy(
+                        out=gw[:, half * 512 : half * 512 + 512].rearrange("p (r m u) -> p r m u", r=2, u=2),
+                        in_=bank[:].rearrange("p r u m -> p r m u"),
+                    )
+                nc.vector.quantize_mx(
+                    out=codes[:, g, :].bitcast(FP8X4),
+                    scales=scales[:, g, :],
+                    in_=grouped[:].rearrange("p d j -> p (d j)"),
+                )
+            KC[h], KS[h] = codes, scales
+
+        def prep_v(h):
+            vp = work.tile([P, PACK, N], BF16, name="vp", align_bytes=64)
+            for s in range(PACK):
+                nc.vector.tensor_tensor(out=vp[:, s, :], in0=V[h][:, s, :].bitcast(FP8), in1=scale[:], op=ALU.mult)
+            words = vp[:].bitcast(F32)
+            codes = work.tile([P, NP, DV], U32, name="vcodes", align_bytes=64)
+            scales = work.tile([P, NP, DV], U8, name="vscales", align_bytes=64)
+            for g in range(NP):
+                grouped = work.tile([P, DV, PACK], BF16, name="vg", align_bytes=64)
+                gw = grouped[:].rearrange("p d j -> p (d j)").bitcast(F32)
+                for half in range(2):
+                    bank = psum.tile([P, 2, 2, P], F32, name="tr", bufs=3)
+                    for r in range(2):
+                        s = 2 * half + r
+                        for u in range(2):
+                            nc.tensor.transpose(
+                                bank[:, r, u, :], words[:, s, 256 * g + u : 256 * (g + 1) : 2], ident[:]
+                            )
+                    nc.scalar.copy(
+                        out=gw[:, half * 512 : half * 512 + 512].rearrange("p (r m u) -> p r m u", r=2, u=2),
+                        in_=bank[:].rearrange("p r u m -> p r m u"),
+                    )
+                nc.vector.quantize_mx(
+                    out=codes[:, g, :].bitcast(FP8X4),
+                    scales=scales[:, g, :],
+                    in_=grouped[:].rearrange("p d j -> p (d j)"),
+                )
+            VC[h], VS[h] = codes, scales
+
+        def prep_q(h):
+            qg = work.tile([P, N, PACK], BF16, name="qg", align_bytes=64)
+            codes = work.tile([P, N], U32, name="qcodes", align_bytes=64)
+            scales = work.tile([P, N], U8, name="qscales", align_bytes=64)
+            for half in range(2):
+                cols = slice(half * 512, half * 512 + 512)
+                dst = qg[:, cols, :].rearrange("p (c i) j -> p c j i", i=4)
+                src = Q[h][:, :, cols].rearrange("p j (c i) -> p c j i", i=4)
+                if half == 0:
+                    nc.vector.tensor_scalar(out=dst, in0=src, scalar1=0.0, scalar2=None, op0=ALU.max)
+                else:
+                    nc.scalar.activation(out=dst, in_=src, func=ACT.Relu)
+                nc.vector.quantize_mx(
+                    out=codes[:, cols].bitcast(FP8X4),
+                    scales=scales[:, cols],
+                    in_=qg[:, cols, :].rearrange("p n j -> p (n j)"),
+                )
+            QG[h], QC[h], QS[h] = qg, codes, scales
+
+        def state(h):
+            vkg = work.tile([P, DV, PACK], BF16, name="vkg", align_bytes=64)
+            codes = work.tile([P, DV], U32, name="vkcodes", align_bytes=64)
+            scales = work.tile([P, DV], U8, name="vkscales", align_bytes=64)
+            for s in range(PACK):
+                bank = psum.tile([P, PACK, P], F32, name="vk", bufs=2)
+                cols = slice(s * P, s * P + P)
+                for t in range(PACK):
+                    rows = slice(t * P, t * P + P)
+                    for g in range(NP):
+                        nc.tensor.matmul_mx(
+                            out=bank[:, t, :],
+                            lhsT=KC[h][:, g, rows].bitcast(FP8X4),
+                            lhsT_scale=KS[h][:, g, rows],
+                            rhs=VC[h][:, g, cols].bitcast(FP8X4),
+                            rhs_scale=VS[h][:, g, cols],
+                            start=(g == 0),
+                            stop=(g == NP - 1),
+                        )
+                nc.scalar.copy(out=vkg[:, cols, :], in_=bank[:].rearrange("p t d -> p d t"))
+            nc.vector.quantize_mx(
+                out=codes[:].bitcast(FP8X4), scales=scales[:], in_=vkg[:].rearrange("p d t -> p (d t)")
+            )
+            VKC[h], VKS[h] = codes, scales
+
+        def norm(h):
+            parts = work.tile([P, PACK, 4], BF16, name="parts")
+            rest1 = work.tile([P, PACK], F32, name="rest1")
+            rest2 = work.tile([P, PACK], F32, name="rest2")
+            nc.gpsimd.tensor_copy(out=parts[:, :, 0], in_=KSUM[h][:])
+            nc.gpsimd.tensor_tensor(out=rest1[:], in0=KSUM[h][:], in1=parts[:, :, 0], op=ALU.subtract)
+            nc.gpsimd.tensor_copy(out=parts[:, :, 1], in_=rest1[:])
+            nc.gpsimd.tensor_tensor(out=rest2[:], in0=rest1[:], in1=parts[:, :, 1], op=ALU.subtract)
+            nc.gpsimd.tensor_copy(out=parts[:, :, 2], in_=rest2[:])
+            den_ps = psum.tile([P, N // P, 4], F32, name="tr", bufs=3)
+            for i in range(N // P):
+                for j in range(PACK):
+                    nc.tensor.matmul(
+                        den_ps[:, i, 0:3],
+                        lhsT=QG[h][:, i * P : i * P + P, j],
+                        rhs=parts[:, j, 0:3],
+                        start=(j == 0),
+                        stop=(j == PACK - 1),
+                    )
+            den = work.tile([P, N // P], F32, name="den")
+            rden = work.tile([P, N // P], F32, name="rden")
+            nc.vector.tensor_reduce(out=den[:], in_=den_ps[:, :, 0:3], axis=AX.X, op=ALU.add)
+            nc.vector.reciprocal(out=rden[:], in_=den[:])
+            rb = work.tile([P, N], F32, name="rb")
+            for half in range(2):
+                bank = psum.tile([P, 4, P], F32, name="tr", bufs=3)
+                for i in range(4):
+                    c = 4 * half + i
+                    nc.tensor.transpose(bank[:, i, :], rden[:, c : c + 1].to_broadcast([P, P]), ident[:])
+                nc.scalar.copy(out=rb[:, half * 512 : half * 512 + 512], in_=bank[:].rearrange("p i n -> p (i n)"))
+            RB[h] = rb
+
+        def apply(h):
+            for s in range(PACK):
+                res = work.tile([P, N], F32, name="res", bufs=3)
+                for half in range(2):
+                    cols = slice(half * 512, half * 512 + 512)
+                    bank = psum.tile([P, 512], F32, name="num", bufs=3)
+                    nc.tensor.matmul_mx(
+                        out=bank[:],
+                        lhsT=VKC[h][:, s * P : s * P + P].bitcast(FP8X4),
+                        lhsT_scale=VKS[h][:, s * P : s * P + P],
+                        rhs=QC[h][:, cols].bitcast(FP8X4),
+                        rhs_scale=QS[h][:, cols],
+                        start=True,
+                        stop=True,
+                    )
+                    nc.vector.tensor_tensor(out=res[:, cols], in0=bank[:], in1=RB[h][:, cols], op=ALU.mult)
+                nc.sync.dma_start(out=out_v[s, h // 2, h % 2], in_=res[:])
+
+        nc.scalar.dma_start(out=scale[:], in_=sc_v.partition_broadcast(P))
+        load_v(0)
+        load_k(0)
+        load_q(0)
+        for h in range(1, H):
+            load_k(h)
+            load_v(h)
+            load_q(h)
+        prep_k(0)
+        prep_v(0)
+        for h in range(H):
+            prep_q(h)
+            state(h)
+            norm(h)
+            if h + 1 < H:
+                prep_k(h + 1)
+                prep_v(h + 1)
+            apply(h)

@@ -27,11 +27,11 @@ def tile_relu_linear_att_pa_kernel(tc, q, k, v_bytes, v_scale, out):
     v_v = v_bytes[0].rearrange("h (m s) n -> h m s n", s=PACK)
     q_v = q[0].rearrange("h (p j) n -> h p j n", j=PACK)
     out_v = out[0].rearrange("(m s a) (b n) -> s a b m n", s=PACK, a=2, b=2)
-    sc_v = v_scale.rearrange("a b c n -> (a b c n)")
+    sc_v = v_scale[0, 0].rearrange("c (p i) -> (c p) i", i=N // P)
 
     with ExitStack() as ctx:
         keep = ctx.enter_context(tc.tile_pool(name="keep", bufs=1))
-        ld = ctx.enter_context(tc.tile_pool(name="ld", bufs=4))
+        ld = ctx.enter_context(tc.tile_pool(name="ld", bufs=3))
         work = ctx.enter_context(tc.tile_pool(name="work", bufs=2))
         psum = ctx.enter_context(tc.psum_pool(name="psum", bufs=1))
 
@@ -41,207 +41,317 @@ def tile_relu_linear_att_pa_kernel(tc, q, k, v_bytes, v_scale, out):
         nc.vector.memset(warm[:], 0.0)
         nc.scalar.activation(out=warm[:], in_=warm[:], func=ACT.Relu)
 
-        scale = keep.tile([P, N], F32, name="scale")
+        scale = keep.tile([P, N], F32, name="scale", align_bytes=64)
+        scol = keep.tile([P, N // P], F32, name="scol")
 
-        K, V, Q, KC, KS, VC, VS, KSUM = {}, {}, {}, {}, {}, {}, {}, {}
-        QG, QC, QS, VKC, VKS, RB = {}, {}, {}, {}, {}, {}
+        raw_k, raw_v, raw_q = {}, {}, {}
+        kr, ksum, parts, vp = {}, {}, {}, {}
+        kcodes, kscales, kgroup = {}, {}, {}
+        vcodes, vscales, vgroup = {}, {}, {}
+        qg, qcodes, qscales = {}, {}, {}
+        vkg, vkcodes, vkscales = {}, {}, {}
+        den_ps, rden, rb, res = {}, {}, {}, {}
+        num_ps, tr_ps = {}, {}
 
-        def load_k(h):
+        def alloc_loads(h):
             t_k = ld.tile([P, PACK, N], BF16, name="t_k")
-            if h == 0:
-                for t in range(PACK):
-                    nc.sync.dma_start(out=t_k[:, t, :], in_=k_v[h][:, t, :])
-            else:
-                nc.sync.dma_start(out=t_k[:], in_=k_v[h])
-            K[h] = t_k
-
-        def load_v(h):
             t_v = ld.tile([P, PACK, N], U8, name="t_v")
-            if h == 0:
-                for s in range(PACK):
-                    nc.sync.dma_start(out=t_v[:, s, :], in_=v_v[h][:, s, :])
-            else:
-                nc.sync.dma_start(out=t_v[:], in_=v_v[h])
-            V[h] = t_v
-
-        def load_q(h):
             t_q = ld.tile([P, PACK, N], BF16, name="t_q")
-            nc.sync.dma_start(out=t_q[:], in_=q_v[h])
-            Q[h] = t_q
+            raw_k[h], raw_v[h], raw_q[h] = t_k, t_v, t_q
 
-        def prep_k(h):
-            kr = work.tile([P, PACK, N], BF16, name="kr", align_bytes=64)
-            ksum = work.tile([P, PACK], F32, name="ksum")
-            for t in range(PACK):
-                nc.scalar.activation(
-                    out=kr[:, t, :].rearrange("m (u x e) -> m u x e", u=2, e=2),
-                    in_=K[h][:, t, :].rearrange("m (x u e) -> m u x e", u=2, e=2),
-                    func=ACT.Relu,
-                    accum_out=ksum[:, t : t + 1],
-                )
-            KSUM[h] = ksum
-            words = kr[:].bitcast(F32)
-            codes = work.tile([P, NP, D], U32, name="kcodes", align_bytes=64)
-            scales = work.tile([P, NP, D], U8, name="kscales", align_bytes=64)
-            for g in range(NP):
-                grouped = work.tile([P, D, PACK], BF16, name="kg", align_bytes=64)
-                gw = grouped[:].rearrange("p d j -> p (d j)").bitcast(F32)
-                for half in range(2):
-                    bank = psum.tile([P, 2, 2, P], F32, name="tr", bufs=3)
-                    for r in range(2):
-                        t = 2 * half + r
-                        for u in range(2):
-                            w0 = u * 256 + g * P
-                            nc.tensor.transpose(bank[:, r, u, :], words[:, t, w0 : w0 + P], ident[:])
-                    nc.scalar.copy(
-                        out=gw[:, half * 512 : half * 512 + 512].rearrange("p (r m u) -> p r m u", r=2, u=2),
-                        in_=bank[:].rearrange("p r u m -> p r m u"),
-                    )
-                nc.vector.quantize_mx(
-                    out=codes[:, g, :].bitcast(FP8X4),
-                    scales=scales[:, g, :],
-                    in_=grouped[:].rearrange("p d j -> p (d j)"),
-                )
-            KC[h], KS[h] = codes, scales
+        def alloc_head(h):
+            t_kr = work.tile([P, PACK, N], BF16, name="t_kr", align_bytes=64)
+            t_ksum = work.tile([P, PACK], F32, name="t_ksum")
+            t_vp = work.tile([P, PACK, N], BF16, name="t_vp", align_bytes=64)
+            t_kc = work.tile([P, NP, D], U32, name="t_kc", align_bytes=64)
+            t_ks = work.tile([P, NP, D], U8, name="t_ks", align_bytes=64)
+            t_vc = work.tile([P, NP, DV], U32, name="t_vc", align_bytes=64)
+            t_vs = work.tile([P, NP, DV], U8, name="t_vs", align_bytes=64)
+            t_qg = work.tile([P, N, PACK], BF16, name="t_qg", align_bytes=64)
+            t_qc = work.tile([P, N], U32, name="t_qc", align_bytes=64)
+            t_qs = work.tile([P, N], U8, name="t_qs", align_bytes=64)
+            kr[h], ksum[h], vp[h] = t_kr, t_ksum, t_vp
+            kcodes[h], kscales[h], vcodes[h], vscales[h] = t_kc, t_ks, t_vc, t_vs
+            qg[h], qcodes[h], qscales[h] = t_qg, t_qc, t_qs
 
-        def prep_v(h):
-            vp = work.tile([P, PACK, N], BF16, name="vp", align_bytes=64)
-            for s in range(PACK):
-                nc.vector.tensor_tensor(out=vp[:, s, :], in0=V[h][:, s, :].bitcast(FP8), in1=scale[:], op=ALU.mult)
-            words = vp[:].bitcast(F32)
-            codes = work.tile([P, NP, DV], U32, name="vcodes", align_bytes=64)
-            scales = work.tile([P, NP, DV], U8, name="vscales", align_bytes=64)
-            for g in range(NP):
-                grouped = work.tile([P, DV, PACK], BF16, name="vg", align_bytes=64)
-                gw = grouped[:].rearrange("p d j -> p (d j)").bitcast(F32)
-                for half in range(2):
-                    bank = psum.tile([P, 2, 2, P], F32, name="tr", bufs=3)
-                    for r in range(2):
-                        s = 2 * half + r
-                        for u in range(2):
-                            nc.tensor.transpose(
-                                bank[:, r, u, :], words[:, s, 256 * g + u : 256 * (g + 1) : 2], ident[:]
-                            )
-                    nc.scalar.copy(
-                        out=gw[:, half * 512 : half * 512 + 512].rearrange("p (r m u) -> p r m u", r=2, u=2),
-                        in_=bank[:].rearrange("p r u m -> p r m u"),
-                    )
-                nc.vector.quantize_mx(
-                    out=codes[:, g, :].bitcast(FP8X4),
-                    scales=scales[:, g, :],
-                    in_=grouped[:].rearrange("p d j -> p (d j)"),
-                )
-            VC[h], VS[h] = codes, scales
-
-        def prep_q(h):
-            qg = work.tile([P, N, PACK], BF16, name="qg", align_bytes=64)
-            codes = work.tile([P, N], U32, name="qcodes", align_bytes=64)
-            scales = work.tile([P, N], U8, name="qscales", align_bytes=64)
-            for half in range(2):
-                cols = slice(half * 512, half * 512 + 512)
-                dst = qg[:, cols, :].rearrange("p (c i) j -> p c j i", i=4)
-                src = Q[h][:, :, cols].rearrange("p j (c i) -> p c j i", i=4)
-                if half == 0:
-                    nc.vector.tensor_scalar(out=dst, in0=src, scalar1=0.0, scalar2=None, op0=ALU.max)
-                else:
-                    nc.scalar.activation(out=dst, in_=src, func=ACT.Relu)
-                nc.vector.quantize_mx(
-                    out=codes[:, cols].bitcast(FP8X4),
-                    scales=scales[:, cols],
-                    in_=qg[:, cols, :].rearrange("p n j -> p (n j)"),
-                )
-            QG[h], QC[h], QS[h] = qg, codes, scales
-
-        def state(h):
-            vkg = work.tile([P, DV, PACK], BF16, name="vkg", align_bytes=64)
-            codes = work.tile([P, DV], U32, name="vkcodes", align_bytes=64)
-            scales = work.tile([P, DV], U8, name="vkscales", align_bytes=64)
-            for s in range(PACK):
-                bank = psum.tile([P, PACK, P], F32, name="vk", bufs=2)
-                cols = slice(s * P, s * P + P)
-                for t in range(PACK):
-                    rows = slice(t * P, t * P + P)
-                    for g in range(NP):
-                        nc.tensor.matmul_mx(
-                            out=bank[:, t, :],
-                            lhsT=KC[h][:, g, rows].bitcast(FP8X4),
-                            lhsT_scale=KS[h][:, g, rows],
-                            rhs=VC[h][:, g, cols].bitcast(FP8X4),
-                            rhs_scale=VS[h][:, g, cols],
-                            start=(g == 0),
-                            stop=(g == NP - 1),
-                        )
-                nc.scalar.copy(out=vkg[:, cols, :], in_=bank[:].rearrange("p t d -> p d t"))
-            nc.vector.quantize_mx(
-                out=codes[:].bitcast(FP8X4), scales=scales[:], in_=vkg[:].rearrange("p d t -> p (d t)")
+        def relu_k(h, t):
+            nc.scalar.activation(
+                out=kr[h][:, t, :].rearrange("m (u x e) -> m u x e", u=2, e=2),
+                in_=raw_k[h][:, t, :].rearrange("m (x u e) -> m u x e", u=2, e=2),
+                func=ACT.Relu,
+                accum_out=ksum[h][:, t : t + 1],
             )
-            VKC[h], VKS[h] = codes, scales
 
-        def norm(h):
-            parts = work.tile([P, PACK, 4], BF16, name="parts")
+        def split_ksum(h):
+            t_parts = work.tile([P, PACK, 4], BF16, name="t_parts")
             rest1 = work.tile([P, PACK], F32, name="rest1")
             rest2 = work.tile([P, PACK], F32, name="rest2")
-            nc.gpsimd.tensor_copy(out=parts[:, :, 0], in_=KSUM[h][:])
-            nc.gpsimd.tensor_tensor(out=rest1[:], in0=KSUM[h][:], in1=parts[:, :, 0], op=ALU.subtract)
-            nc.gpsimd.tensor_copy(out=parts[:, :, 1], in_=rest1[:])
-            nc.gpsimd.tensor_tensor(out=rest2[:], in0=rest1[:], in1=parts[:, :, 1], op=ALU.subtract)
-            nc.gpsimd.tensor_copy(out=parts[:, :, 2], in_=rest2[:])
-            den_ps = psum.tile([P, N // P, 4], F32, name="tr", bufs=3)
-            for i in range(N // P):
+            nc.gpsimd.tensor_copy(out=t_parts[:, :, 0], in_=ksum[h][:])
+            nc.gpsimd.tensor_tensor(out=rest1[:], in0=ksum[h][:], in1=t_parts[:, :, 0], op=ALU.subtract)
+            nc.gpsimd.tensor_copy(out=t_parts[:, :, 1], in_=rest1[:])
+            nc.gpsimd.tensor_tensor(out=rest2[:], in0=rest1[:], in1=t_parts[:, :, 1], op=ALU.subtract)
+            nc.gpsimd.tensor_copy(out=t_parts[:, :, 2], in_=rest2[:])
+            parts[h] = t_parts
+
+        def spread_scale():
+            for b in range(2):
+                bank = psum.tile([P, 4, P], F32, name="tr", bufs=3)
+                for i in range(4):
+                    c = 4 * b + i
+                    nc.tensor.transpose(bank[:, i, :], scol[:, c : c + 1].to_broadcast([P, P]), ident[:])
+                nc.vector.tensor_copy(
+                    out=scale[:].rearrange("m (p b i) -> m b p i", b=2, i=4)[:, b], in_=bank[:].rearrange("m i p -> m p i")
+                )
+
+        def prod_v(h, s):
+            nc.vector.tensor_tensor(out=vp[h][:, s, :], in0=raw_v[h][:, s, :].bitcast(FP8), in1=scale[:], op=ALU.mult)
+
+        def turn(kind, h, g, half):
+            words = (kr if kind == "k" else vp)[h][:].bitcast(F32)
+            bank = psum.tile([P, 2, 2, P], F32, name="tr", bufs=3)
+            for r in range(2):
+                for u in range(2):
+                    if kind == "k":
+                        cols = slice(u * 256 + g * P, u * 256 + g * P + P)
+                    else:
+                        cols = slice(256 * g + u, 256 * (g + 1), 2)
+                    nc.tensor.transpose(bank[:, r, u, :], words[:, 2 * half + r, cols], ident[:])
+            group = kgroup if kind == "k" else vgroup
+            if (h, g) not in group:
+                grouped = work.tile([P, D, PACK], BF16, name="grouped", align_bytes=64, bufs=4)
+                group[h, g] = grouped
+            gw = group[h, g][:].rearrange("p d j -> p (d j)").bitcast(F32)
+            nc.scalar.copy(
+                out=gw[:, half * 512 : half * 512 + 512].rearrange("p (r m u) -> p r m u", r=2, u=2),
+                in_=bank[:].rearrange("p r u m -> p r m u"),
+            )
+
+        def quant_k(h, g):
+            nc.vector.quantize_mx(
+                out=kcodes[h][:, g, :].bitcast(FP8X4),
+                scales=kscales[h][:, g, :],
+                in_=kgroup[h, g][:].rearrange("p d j -> p (d j)"),
+            )
+
+        def quant_v(h, g):
+            nc.vector.quantize_mx(
+                out=vcodes[h][:, g, :].bitcast(FP8X4),
+                scales=vscales[h][:, g, :],
+                in_=vgroup[h, g][:].rearrange("p d j -> p (d j)"),
+            )
+
+        def relu_q(h, eng, n0, n1):
+            dst = qg[h][:, n0:n1, :].rearrange("p (c i) j -> p c j i", i=4)
+            src = raw_q[h][:, :, n0:n1].rearrange("p j (c i) -> p c j i", i=4)
+            if eng == "v":
+                nc.vector.tensor_scalar(out=dst, in0=src, scalar1=0.0, scalar2=None, op0=ALU.max)
+            else:
+                nc.scalar.activation(out=dst, in_=src, func=ACT.Relu)
+
+        def quant_q(h, half):
+            cols = slice(half * 512, half * 512 + 512)
+            nc.vector.quantize_mx(
+                out=qcodes[h][:, cols].bitcast(FP8X4),
+                scales=qscales[h][:, cols],
+                in_=qg[h][:, cols, :].rearrange("p n j -> p (n j)"),
+            )
+
+        def den_mm(h, i0, i1):
+            if h not in den_ps:
+                t_den = psum.tile([P, N // P, 4], F32, name="dn", bufs=1)
+                den_ps[h] = t_den
+            for i in range(i0, i1):
                 for j in range(PACK):
                     nc.tensor.matmul(
-                        den_ps[:, i, 0:3],
-                        lhsT=QG[h][:, i * P : i * P + P, j],
-                        rhs=parts[:, j, 0:3],
+                        den_ps[h][:, i, 0:3],
+                        lhsT=qg[h][:, i * P : i * P + P, j],
+                        rhs=parts[h][:, j, 0:3],
                         start=(j == 0),
                         stop=(j == PACK - 1),
                     )
+
+        def recip(h):
             den = work.tile([P, N // P], F32, name="den")
-            rden = work.tile([P, N // P], F32, name="rden")
-            nc.vector.tensor_reduce(out=den[:], in_=den_ps[:, :, 0:3], axis=AX.X, op=ALU.add)
-            nc.vector.reciprocal(out=rden[:], in_=den[:])
-            rb = work.tile([P, N], F32, name="rb")
+            t_rden = work.tile([P, N // P], F32, name="t_rden")
+            nc.vector.tensor_reduce(out=den[:], in_=den_ps[h][:, :, 0:3], axis=AX.X, op=ALU.add)
+            nc.vector.reciprocal(out=t_rden[:], in_=den[:])
+            rden[h] = t_rden
+
+        def spread(h):
+            t_rb = work.tile([P, N], F32, name="t_rb")
+            rb[h] = t_rb
             for half in range(2):
                 bank = psum.tile([P, 4, P], F32, name="tr", bufs=3)
                 for i in range(4):
                     c = 4 * half + i
-                    nc.tensor.transpose(bank[:, i, :], rden[:, c : c + 1].to_broadcast([P, P]), ident[:])
-                nc.scalar.copy(out=rb[:, half * 512 : half * 512 + 512], in_=bank[:].rearrange("p i n -> p (i n)"))
-            RB[h] = rb
+                    nc.tensor.transpose(bank[:, i, :], rden[h][:, c : c + 1].to_broadcast([P, P]), ident[:])
+                nc.scalar.copy(out=t_rb[:, half * 512 : half * 512 + 512], in_=bank[:].rearrange("p i n -> p (i n)"))
 
-        def apply(h):
-            for s in range(PACK):
-                res = work.tile([P, N], F32, name="res", bufs=3)
-                for half in range(2):
-                    cols = slice(half * 512, half * 512 + 512)
-                    bank = psum.tile([P, 512], F32, name="num", bufs=3)
+        def state(h, s):
+            if s == 0:
+                t_vkg = work.tile([P, DV, PACK], BF16, name="t_vkg", align_bytes=64)
+                t_vkc = work.tile([P, DV], U32, name="t_vkc", align_bytes=64)
+                t_vks = work.tile([P, DV], U8, name="t_vks", align_bytes=64)
+                vkg[h], vkcodes[h], vkscales[h] = t_vkg, t_vkc, t_vks
+            bank = psum.tile([P, PACK, P], F32, name="mm", bufs=4)
+            cols = slice(s * P, s * P + P)
+            for t in range(PACK):
+                rows = slice(t * P, t * P + P)
+                for g in range(NP):
                     nc.tensor.matmul_mx(
-                        out=bank[:],
-                        lhsT=VKC[h][:, s * P : s * P + P].bitcast(FP8X4),
-                        lhsT_scale=VKS[h][:, s * P : s * P + P],
-                        rhs=QC[h][:, cols].bitcast(FP8X4),
-                        rhs_scale=QS[h][:, cols],
-                        start=True,
-                        stop=True,
+                        out=bank[:, t, :],
+                        lhsT=kcodes[h][:, g, rows].bitcast(FP8X4),
+                        lhsT_scale=kscales[h][:, g, rows],
+                        rhs=vcodes[h][:, g, cols].bitcast(FP8X4),
+                        rhs_scale=vscales[h][:, g, cols],
+                        start=(g == 0),
+                        stop=(g == NP - 1),
                     )
-                    nc.vector.tensor_tensor(out=res[:, cols], in0=bank[:], in1=RB[h][:, cols], op=ALU.mult)
-                nc.sync.dma_start(out=out_v[s, h // 2, h % 2], in_=res[:])
+            nc.scalar.copy(out=vkg[h][:, cols, :], in_=bank[:].rearrange("p t d -> p d t"))
 
-        nc.scalar.dma_start(out=scale[:], in_=sc_v.partition_broadcast(P))
-        load_v(0)
-        load_k(0)
-        load_q(0)
-        for h in range(1, H):
-            load_k(h)
-            load_v(h)
-            load_q(h)
-        prep_k(0)
-        prep_v(0)
+        def quant_state(h, half):
+            cols = slice(256 * half, 256 * half + 256)
+            nc.vector.quantize_mx(
+                out=vkcodes[h][:, cols].bitcast(FP8X4),
+                scales=vkscales[h][:, cols],
+                in_=vkg[h][:, cols, :].rearrange("p d t -> p (d t)"),
+            )
+
+        def num(h, x):
+            s, half = divmod(x, 2)
+            cols = slice(half * 512, half * 512 + 512)
+            bank = psum.tile([P, 512], F32, name="mm", bufs=4)
+            nc.tensor.matmul_mx(
+                out=bank[:],
+                lhsT=vkcodes[h][:, s * P : s * P + P].bitcast(FP8X4),
+                lhsT_scale=vkscales[h][:, s * P : s * P + P],
+                rhs=qcodes[h][:, cols].bitcast(FP8X4),
+                rhs_scale=qscales[h][:, cols],
+                start=True,
+                stop=True,
+            )
+            num_ps[h, x] = bank
+
+        def mult(h, x):
+            s, half = divmod(x, 2)
+            cols = slice(half * 512, half * 512 + 512)
+            if half == 0:
+                t_res = work.tile([P, N], F32, name="t_res", bufs=4)
+                res[h, s] = t_res
+            nc.vector.tensor_tensor(out=res[h, s][:, cols], in0=num_ps[h, x][:], in1=rb[h][:, cols], op=ALU.mult)
+            if half == 1:
+                nc.sync.dma_start(out=out_v[s, h // 2, h % 2], in_=res[h, s][:])
+
+        ctx.enter_context(tc.manual_schedule())
+
         for h in range(H):
-            prep_q(h)
-            state(h)
-            norm(h)
-            if h + 1 < H:
-                prep_k(h + 1)
-                prep_v(h + 1)
-            apply(h)
+            alloc_loads(h)
+        nc.scalar.dma_start(out=scol[:], in_=sc_v)
+        nc.sync.dma_start(out=raw_q[0][:, :, 0:256], in_=q_v[0][:, :, 0:256])
+        nc.sync.dma_start(out=raw_k[0][:, 0, :], in_=k_v[0][:, 0, :])
+        nc.sync.dma_start(out=raw_v[0][:, 0:2, :], in_=v_v[0][:, 0:2, :])
+        nc.sync.dma_start(out=raw_k[0][:, 1, :], in_=k_v[0][:, 1, :])
+        nc.sync.dma_start(out=raw_v[0][:, 2:4, :], in_=v_v[0][:, 2:4, :])
+        nc.sync.dma_start(out=raw_k[0][:, 2, :], in_=k_v[0][:, 2, :])
+        nc.sync.dma_start(out=raw_k[0][:, 3, :], in_=k_v[0][:, 3, :])
+        nc.sync.dma_start(out=raw_q[0][:, :, 256:1024], in_=q_v[0][:, :, 256:1024])
+        for h in range(1, H):
+            nc.sync.dma_start(out=raw_v[h][:], in_=v_v[h])
+            nc.sync.dma_start(out=raw_k[h][:], in_=k_v[h])
+            nc.sync.dma_start(out=raw_q[h][:], in_=q_v[h])
+
+        alloc_head(0)
+        relu_q(0, "v", 0, 256)
+        spread_scale()
+        for t in range(PACK):
+            relu_k(0, t)
+        split_ksum(0)
+        prod_v(0, 0)
+        prod_v(0, 1)
+        turn("k", 0, 0, 0)
+        turn("k", 0, 1, 0)
+        prod_v(0, 2)
+        prod_v(0, 3)
+        turn("v", 0, 0, 0)
+        turn("v", 0, 1, 0)
+        relu_q(0, "v", 256, 512)
+        turn("k", 0, 0, 1)
+        turn("k", 0, 1, 1)
+        turn("v", 0, 0, 1)
+        turn("v", 0, 1, 1)
+        relu_q(0, "v", 512, 1024)
+        quant_q(0, 0)
+        quant_k(0, 0)
+        quant_k(0, 1)
+        quant_q(0, 1)
+        den_mm(0, 0, 4)
+        quant_v(0, 0)
+        quant_v(0, 1)
+
+        for h in range(H):
+            n = h + 1
+            more = n < H
+            old = h - 1
+            if more:
+                alloc_head(n)
+                for t in range(PACK):
+                    relu_k(n, t)
+                split_ksum(n)
+            den_mm(h, 4, 8)
+            if old >= 0:
+                num(old, 4)
+                num(old, 5)
+            if more:
+                prod_v(n, 0)
+                prod_v(n, 1)
+            recip(h)
+            if old >= 0:
+                mult(old, 4)
+                mult(old, 5)
+            for s in range(PACK):
+                if s == 2 and old >= 0:
+                    num(old, 6)
+                    num(old, 7)
+                state(h, s)
+                if s == 1:
+                    if more:
+                        prod_v(n, 2)
+                    quant_state(h, 0)
+            if more:
+                prod_v(n, 3)
+            if old >= 0:
+                mult(old, 6)
+                mult(old, 7)
+            spread(h)
+            quant_state(h, 1)
+            if more:
+                relu_q(n, "v", 0, 512)
+                turn("v", n, 0, 0)
+                turn("v", n, 0, 1)
+                num(h, 0)
+                num(h, 1)
+                turn("v", n, 1, 0)
+                turn("v", n, 1, 1)
+                mult(h, 0)
+                mult(h, 1)
+                quant_v(n, 0)
+                quant_q(n, 0)
+                relu_q(n, "s", 512, 768)
+                turn("k", n, 0, 0)
+                turn("k", n, 0, 1)
+                quant_v(n, 1)
+                relu_q(n, "s", 768, 1024)
+                num(h, 2)
+                num(h, 3)
+                den_mm(n, 0, 4)
+                turn("k", n, 1, 0)
+                turn("k", n, 1, 1)
+                mult(h, 2)
+                quant_k(n, 0)
+                mult(h, 3)
+                quant_q(n, 1)
+                quant_k(n, 1)
+            else:
+                for x in range(8):
+                    num(h, x)
+                    mult(h, x)

@@ -20,6 +20,69 @@ PASS = P * PACK
 NP = N // PASS
 FLOPS = 2 * 2 * H * D * DV * N
 
+PROLOGUE = [
+    ('scale', ()),
+    ('prod', (2,)),
+]
+PERIOD = [
+    ('den', 2, ()),
+    ('recip', 2, ()),
+    ('il', 2, (0,)),
+    ('quant', 1, ('k', 0)),
+    ('state', 2, (0,)),
+    ('num', 3, (4,)),
+    ('turn', 1, ('v', 0, 1)),
+    ('rt', 2, ()),
+    ('turn', 1, ('v', 1, 1)),
+    ('num', 3, (2,)),
+    ('state', 2, (1,)),
+    ('ks1', 1, ()),
+    ('mult', 3, (4,)),
+    ('prod', 1, (1,)),
+    ('rq', 1, (1,)),
+    ('mult', 3, (2,)),
+    ('il', 2, (3,)),
+    ('num', 3, (3,)),
+    ('num', 3, (5,)),
+    ('quant_q', 2, (0,)),
+    ('il', 1, (2,)),
+    ('prod', 0, (3,)),
+    ('mult', 3, (3,)),
+    ('state', 2, (2,)),
+    ('turn', 0, ('k', 1, 0)),
+    ('ks2', 1, ()),
+    ('quant', 1, ('k', 1)),
+    ('turn', 1, ('v', 0, 0)),
+    ('ks3', 1, ()),
+    ('quant_s', 2, (0,)),
+    ('quant_q', 2, (1,)),
+    ('mult', 3, (5,)),
+    ('num', 3, (6,)),
+    ('rq', 0, (0,)),
+    ('state', 2, (3,)),
+    ('ks4', 1, ()),
+    ('num', 3, (7,)),
+    ('turn', 1, ('v', 1, 0)),
+    ('turn', 0, ('k', 0, 1)),
+    ('turn', 0, ('k', 0, 0)),
+    ('mult', 3, (6,)),
+    ('split', 1, ()),
+    ('prod', 0, (2,)),
+    ('turn', 0, ('k', 1, 1)),
+    ('quant', 1, ('v', 0)),
+    ('num', 2, (0,)),
+    ('num', 2, (1,)),
+    ('il', 1, (1,)),
+    ('mult', 3, (7,)),
+    ('quant_s', 2, (1,)),
+    ('quant', 1, ('v', 1)),
+    ('prod', 0, (0,)),
+    ('mult', 2, (0,)),
+    ('mult', 2, (1,)),
+]
+VECTOR_IL = {(0, 1), (1, 2), (3, 0)}
+GPSIMD_MULT = {4}
+
 
 def tile_relu_linear_att_pa_kernel(tc, q, k, v_bytes, v_scale, out):
     nc = tc.nc
@@ -31,327 +94,283 @@ def tile_relu_linear_att_pa_kernel(tc, q, k, v_bytes, v_scale, out):
 
     with ExitStack() as ctx:
         keep = ctx.enter_context(tc.tile_pool(name="keep", bufs=1))
-        ld = ctx.enter_context(tc.tile_pool(name="ld", bufs=3))
+        ld = ctx.enter_context(tc.tile_pool(name="ld", bufs=4))
         work = ctx.enter_context(tc.tile_pool(name="work", bufs=2))
-        psum = ctx.enter_context(tc.psum_pool(name="psum", bufs=1))
+        psum = ctx.enter_context(tc.psum_pool(name="psum", bufs=4))
 
         ident = keep.tile([P, P], F32, name="ident")
         make_identity(nc, ident[:])
         warm = keep.tile([P, 1], F32, name="warm")
         nc.vector.memset(warm[:], 0.0)
         nc.scalar.activation(out=warm[:], in_=warm[:], func=ACT.Relu)
-
+        ones = keep.tile([P, 1], BF16, name="ones")
+        nc.vector.memset(ones[:], 1.0)
+        quad = keep.tile([P, 32], F32, name="quad")
+        sel = keep.tile([P, PACK, P], F32, name="sel")
+        rden = keep.tile([P, 2, P], F32, name="rden")
+        nc.gpsimd.memset(sel[:], 0.0)
+        nc.gpsimd.memset(rden[:], 0.0)
         scale = keep.tile([P, N], F32, name="scale", align_bytes=64)
         scol = keep.tile([P, N // P], F32, name="scol")
 
-        raw_k, raw_v, raw_q = {}, {}, {}
-        kr, ksum, parts, vp = {}, {}, {}, {}
-        kcodes, kscales, kgroup = {}, {}, {}
-        vcodes, vscales, vgroup = {}, {}, {}
-        qg, qcodes, qscales = {}, {}, {}
-        vkg, vkcodes, vkscales = {}, {}, {}
-        den_ps, rden, rb, res = {}, {}, {}, {}
-        num_ps, tr_ps = {}, {}
+        ctx.enter_context(tc.manual_schedule())
 
-        def alloc_loads(h):
+        nc.vector.tensor_reduce(out=quad[:], in_=ident[:].rearrange("p (c j) -> p c j", j=PACK), axis=AX.X, op=ALU.add)
+        for b in range(PACK):
+            nc.gpsimd.tensor_copy(out=sel[:, b, 32 * b : 32 * b + 32], in_=quad[:])
+
+        raw_k, raw_v, raw_q = [], [], []
+        for h in range(H):
             t_k = ld.tile([P, PACK, N], BF16, name="t_k")
             t_v = ld.tile([P, PACK, N], U8, name="t_v")
             t_q = ld.tile([P, PACK, N], BF16, name="t_q")
-            raw_k[h], raw_v[h], raw_q[h] = t_k, t_v, t_q
+            raw_k.append(t_k)
+            raw_v.append(t_v)
+            raw_q.append(t_q)
+        nc.scalar.dma_start(out=scol[:], in_=sc_v)
+        for c in range(2):
+            nc.sync.dma_start(out=raw_v[0][:, 2 * c : 2 * c + 2, :], in_=v_v[0][:, 2 * c : 2 * c + 2, :])
+            nc.sync.dma_start(out=raw_k[0][:, 2 * c : 2 * c + 2, :], in_=k_v[0][:, 2 * c : 2 * c + 2, :])
+        for c in range(2):
+            nc.sync.dma_start(out=raw_q[0][:, :, 512 * c : 512 * c + 512], in_=q_v[0][:, :, 512 * c : 512 * c + 512])
+        for h in range(1, H):
+            nc.sync.dma_start(out=raw_k[h][:], in_=k_v[h])
+            nc.sync.dma_start(out=raw_v[h][:], in_=v_v[h])
+            nc.sync.dma_start(out=raw_q[h][:], in_=q_v[h])
 
-        def alloc_head(h):
-            t_kr = work.tile([P, PACK, N], BF16, name="t_kr", align_bytes=64)
-            t_ksum = work.tile([P, PACK], F32, name="t_ksum")
-            t_vp = work.tile([P, PACK, N], BF16, name="t_vp", align_bytes=64)
-            t_kc = work.tile([P, NP, D], U32, name="t_kc", align_bytes=64)
-            t_ks = work.tile([P, NP, D], U8, name="t_ks", align_bytes=64)
-            t_vc = work.tile([P, NP, DV], U32, name="t_vc", align_bytes=64)
-            t_vs = work.tile([P, NP, DV], U8, name="t_vs", align_bytes=64)
-            t_qg = work.tile([P, N, PACK], BF16, name="t_qg", align_bytes=64)
-            t_qc = work.tile([P, N], U32, name="t_qc", align_bytes=64)
-            t_qs = work.tile([P, N], U8, name="t_qs", align_bytes=64)
-            kr[h], ksum[h], vp[h] = t_kr, t_ksum, t_vp
-            kcodes[h], kscales[h], vcodes[h], vscales[h] = t_kc, t_ks, t_vc, t_vs
-            qg[h], qcodes[h], qscales[h] = t_qg, t_qc, t_qs
+        made = {}
 
-        def relu_k(h, t):
-            nc.scalar.activation(
-                out=kr[h][:, t, :].rearrange("m (u x e) -> m u x e", u=2, e=2),
-                in_=raw_k[h][:, t, :].rearrange("m (x u e) -> m u x e", u=2, e=2),
-                func=ACT.Relu,
-                accum_out=ksum[h][:, t : t + 1],
-            )
+        def sbuf(key, shape, dtype, bufs=2):
+            if key not in made:
+                t = work.tile(shape, dtype, name=key[0], align_bytes=64, bufs=bufs)
+                made[key] = t
+            return made[key]
 
-        def split_ksum(h):
-            t_parts = work.tile([P, PACK, 4], BF16, name="t_parts")
-            rest1 = work.tile([P, PACK], F32, name="rest1")
-            rest2 = work.tile([P, PACK], F32, name="rest2")
-            nc.gpsimd.tensor_copy(out=t_parts[:, :, 0], in_=ksum[h][:])
-            nc.gpsimd.tensor_tensor(out=rest1[:], in0=ksum[h][:], in1=t_parts[:, :, 0], op=ALU.subtract)
-            nc.gpsimd.tensor_copy(out=t_parts[:, :, 1], in_=rest1[:])
-            nc.gpsimd.tensor_tensor(out=rest2[:], in0=rest1[:], in1=t_parts[:, :, 1], op=ALU.subtract)
-            nc.gpsimd.tensor_copy(out=t_parts[:, :, 2], in_=rest2[:])
-            parts[h] = t_parts
+        def bank(key, tag, shape):
+            if key not in made:
+                t = psum.tile(shape, F32, name=tag)
+                made[key] = t
+            return made[key]
 
-        def spread_scale():
+        def spread_scale(h):
             for b in range(2):
-                bank = psum.tile([P, 4, P], F32, name="tr", bufs=3)
+                t = psum.tile([P, 4, P], F32, name="tr")
                 for i in range(4):
                     c = 4 * b + i
-                    nc.tensor.transpose(bank[:, i, :], scol[:, c : c + 1].to_broadcast([P, P]), ident[:])
+                    nc.tensor.transpose(t[:, i, :], scol[:, c : c + 1].to_broadcast([P, P]), ident[:])
                 nc.vector.tensor_copy(
-                    out=scale[:].rearrange("m (p b i) -> m b p i", b=2, i=4)[:, b], in_=bank[:].rearrange("m i p -> m p i")
+                    out=scale[:].rearrange("m (p b i) -> m b p i", b=2, i=4)[:, b], in_=t[:].rearrange("m i p -> m p i")
                 )
 
-        def prod_v(h, s):
-            nc.vector.tensor_tensor(out=vp[h][:, s, :], in0=raw_v[h][:, s, :].bitcast(FP8), in1=scale[:], op=ALU.mult)
+        def prod(h, s):
+            vp = sbuf(("vp", h), [P, PACK, N], BF16)
+            nc.vector.tensor_tensor(out=vp[:, s, :], in0=raw_v[h][:, s, :].bitcast(FP8), in1=scale[:], op=ALU.mult)
 
-        def turn(kind, h, g, half):
-            words = (kr if kind == "k" else vp)[h][:].bitcast(F32)
-            bank = psum.tile([P, 2, 2, P], F32, name="tr", bufs=3)
-            for r in range(2):
-                for u in range(2):
-                    if kind == "k":
-                        cols = slice(u * 256 + g * P, u * 256 + g * P + P)
-                    else:
-                        cols = slice(256 * g + u, 256 * (g + 1), 2)
-                    nc.tensor.transpose(bank[:, r, u, :], words[:, 2 * half + r, cols], ident[:])
-            group = kgroup if kind == "k" else vgroup
-            if (h, g) not in group:
-                grouped = work.tile([P, D, PACK], BF16, name="grouped", align_bytes=64, bufs=4)
-                group[h, g] = grouped
-            gw = group[h, g][:].rearrange("p d j -> p (d j)").bitcast(F32)
-            nc.scalar.copy(
-                out=gw[:, half * 512 : half * 512 + 512].rearrange("p (r m u) -> p r m u", r=2, u=2),
-                in_=bank[:].rearrange("p r u m -> p r m u"),
-            )
+        def relu_q(h, c):
+            rq = sbuf(("rq", h), [P, PACK, N], BF16)
+            cols = slice(512 * c, 512 * c + 512)
+            nc.vector.tensor_scalar(out=rq[:, :, cols], in0=raw_q[h][:, :, cols], scalar1=0.0, scalar2=None, op0=ALU.max)
 
-        def quant_k(h, g):
-            nc.vector.quantize_mx(
-                out=kcodes[h][:, g, :].bitcast(FP8X4),
-                scales=kscales[h][:, g, :],
-                in_=kgroup[h, g][:].rearrange("p d j -> p (d j)"),
-            )
-
-        def quant_v(h, g):
-            nc.vector.quantize_mx(
-                out=vcodes[h][:, g, :].bitcast(FP8X4),
-                scales=vscales[h][:, g, :],
-                in_=vgroup[h, g][:].rearrange("p d j -> p (d j)"),
-            )
-
-        def relu_q(h, eng, n0, n1):
-            dst = qg[h][:, n0:n1, :].rearrange("p (c i) j -> p c j i", i=4)
-            src = raw_q[h][:, :, n0:n1].rearrange("p j (c i) -> p c j i", i=4)
-            if eng == "v":
-                nc.vector.tensor_scalar(out=dst, in0=src, scalar1=0.0, scalar2=None, op0=ALU.max)
+        def interleave(h, c):
+            qg = sbuf(("qg", h), [P, N, PACK], BF16)
+            cols = slice(256 * c, 256 * c + 256)
+            dst = qg[:, cols, :].rearrange("p (c i) j -> p c j i", i=4)
+            src = made["rq", h][:, :, cols].rearrange("p j (c i) -> p c j i", i=4)
+            if (h, c) in VECTOR_IL:
+                nc.vector.tensor_copy(out=dst, in_=src)
             else:
-                nc.scalar.activation(out=dst, in_=src, func=ACT.Relu)
+                nc.scalar.copy(out=dst, in_=src)
 
-        def quant_q(h, half):
-            cols = slice(half * 512, half * 512 + 512)
+        def quant_q(h, c):
+            codes = sbuf(("qc", h), [P, N], U32, 3)
+            planes = sbuf(("qs", h), [P, N], U8, 3)
+            cols = slice(512 * c, 512 * c + 512)
             nc.vector.quantize_mx(
-                out=qcodes[h][:, cols].bitcast(FP8X4),
-                scales=qscales[h][:, cols],
-                in_=qg[h][:, cols, :].rearrange("p n j -> p (n j)"),
+                out=codes[:, cols].bitcast(FP8X4),
+                scales=planes[:, cols],
+                in_=made["qg", h][:, cols, :].rearrange("p n j -> p (n j)"),
             )
 
-        def den_mm(h, i0, i1):
-            if h not in den_ps:
-                t_den = psum.tile([P, N // P, 4], F32, name="dn", bufs=1)
-                den_ps[h] = t_den
-            for i in range(i0, i1):
+        def turn(h, kind, g, half):
+            words = (raw_k[h] if kind == "k" else made["vp", h])[:].bitcast(F32)
+            t = psum.tile([P, 2, 2, P], F32, name="tr")
+            for u in range(2):
+                for r in range(2):
+                    nc.tensor.transpose(t[:, u, r, :], words[:, 2 * half + r, 256 * g + u : 256 * (g + 1) : 2], ident[:])
+            dst = sbuf(("grp", h, kind, g), [P, D, PACK], BF16, 6)[:, 256 * half : 256 * half + 256, :]
+            if kind == "k":
+                nc.scalar.activation(
+                    out=dst.rearrange("p c (u e) -> p c u e", e=2),
+                    in_=t[:].rearrange("p u r m -> p u (r m)").bitcast(BF16).rearrange("p u (c e) -> p c u e", e=2),
+                    func=ACT.Relu,
+                )
+            else:
+                nc.scalar.copy(
+                    out=dst.rearrange("p c j -> p (c j)").bitcast(F32).rearrange("p (c u) -> p c u", u=2),
+                    in_=t[:].rearrange("p u r m -> p (r m) u"),
+                )
+
+        def quant(h, kind, g):
+            codes = sbuf((kind + "c", h), [P, NP, D], U32)
+            planes = sbuf((kind + "s_", h), [P, NP, D], U8)
+            nc.vector.quantize_mx(
+                out=codes[:, g, :].bitcast(FP8X4),
+                scales=planes[:, g, :],
+                in_=made["grp", h, kind, g][:].rearrange("p c j -> p (c j)"),
+            )
+
+        def ks1(h):
+            t = bank(("ks", h), "tr", [P, PASS])
+            for i in range(16):
+                for g in range(NP):
+                    nc.tensor.matmul(
+                        t[:, i : i + 1],
+                        lhsT=made["grp", h, "k", g][:, 32 * i : 32 * i + 32, :].rearrange("p c j -> p (c j)"),
+                        rhs=ones[:],
+                        start=(g == 0),
+                        stop=(g == NP - 1),
+                    )
+
+        def ks2(h):
+            part = sbuf(("part", h), [P, PACK, 4], F32)
+            nc.vector.tensor_copy(out=part[:], in_=made["ks", h][:, 0:16].rearrange("p (t b) -> p t b", b=4))
+
+        def ks3(h):
+            for b in range(4):
+                nc.tensor.matmul(
+                    made["ks", h][:, 16:20], lhsT=sel[:, b, :], rhs=made["part", h][:, :, b], start=(b == 0), stop=(b == 3)
+                )
+
+        def ks4(h):
+            ksum = sbuf(("ksum", h), [P, PACK], F32)
+            nc.vector.tensor_copy(out=ksum[:], in_=made["ks", h][:, 16:20])
+
+        def split(h):
+            ksum = made["ksum", h]
+            parts = sbuf(("parts", h), [P, PACK, 4], BF16)
+            rest1 = sbuf(("rest1", h), [P, PACK], F32)
+            rest2 = sbuf(("rest2", h), [P, PACK], F32)
+            nc.gpsimd.tensor_copy(out=parts[:, :, 0], in_=ksum[:])
+            nc.gpsimd.tensor_tensor(out=rest1[:], in0=ksum[:], in1=parts[:, :, 0], op=ALU.subtract)
+            nc.gpsimd.tensor_copy(out=parts[:, :, 1], in_=rest1[:])
+            nc.gpsimd.tensor_tensor(out=rest2[:], in0=rest1[:], in1=parts[:, :, 1], op=ALU.subtract)
+            nc.gpsimd.tensor_copy(out=parts[:, :, 2], in_=rest2[:])
+
+        def den(h):
+            t = bank(("den", h), "tr", [P, N // P, 4])
+            for i in range(N // P):
                 for j in range(PACK):
                     nc.tensor.matmul(
-                        den_ps[h][:, i, 0:3],
-                        lhsT=qg[h][:, i * P : i * P + P, j],
-                        rhs=parts[h][:, j, 0:3],
+                        t[:, i, 0:3],
+                        lhsT=made["rq", h][:, j, i * P : i * P + P],
+                        rhs=made["parts", h][:, j, 0:3],
                         start=(j == 0),
                         stop=(j == PACK - 1),
                     )
 
         def recip(h):
-            den = work.tile([P, N // P], F32, name="den")
-            t_rden = work.tile([P, N // P], F32, name="t_rden")
-            nc.vector.tensor_reduce(out=den[:], in_=den_ps[h][:, :, 0:3], axis=AX.X, op=ALU.add)
-            nc.vector.reciprocal(out=t_rden[:], in_=den[:])
-            rden[h] = t_rden
+            total = sbuf(("total", h), [P, N // P], F32)
+            nc.vector.tensor_reduce(out=total[:], in_=made["den", h][:, :, 0:3], axis=AX.X, op=ALU.add)
+            nc.vector.reciprocal(out=rden[:, h % 2, 0 : N // P], in_=total[:])
 
-        def spread(h):
-            t_rb = work.tile([P, N], F32, name="t_rb")
-            rb[h] = t_rb
-            for half in range(2):
-                bank = psum.tile([P, 4, P], F32, name="tr", bufs=3)
-                for i in range(4):
-                    c = 4 * half + i
-                    nc.tensor.transpose(bank[:, i, :], rden[h][:, c : c + 1].to_broadcast([P, P]), ident[:])
-                nc.scalar.copy(out=t_rb[:, half * 512 : half * 512 + 512], in_=bank[:].rearrange("p i n -> p (i n)"))
+        def row(h):
+            t = bank(("row", h), "tr", [P, P])
+            nc.tensor.transpose(t[:], rden[:, h % 2, :], ident[:])
+            rrow = sbuf(("rrow", h), [32, P], F32)
+            nc.scalar.copy(out=rrow[:], in_=t[0:32, :])
+            park = out_v[PACK - 1, h // 2, h % 2][0:1, :]
+            nc.sync.dma_start(out=park.rearrange("o (i p) -> (o i) p", p=P), in_=rrow[0 : N // P, :])
+            rb = sbuf(("rb", h), [P, N], F32)
+            nc.sync.dma_start(out=rb[:], in_=park.rearrange("o n -> (o n)").partition_broadcast(P))
 
         def state(h, s):
-            if s == 0:
-                t_vkg = work.tile([P, DV, PACK], BF16, name="t_vkg", align_bytes=64)
-                t_vkc = work.tile([P, DV], U32, name="t_vkc", align_bytes=64)
-                t_vks = work.tile([P, DV], U8, name="t_vks", align_bytes=64)
-                vkg[h], vkcodes[h], vkscales[h] = t_vkg, t_vkc, t_vks
-            bank = psum.tile([P, PACK, P], F32, name="mm", bufs=4)
+            vkg = sbuf(("vkg", h), [P, DV, PACK], BF16)
+            t = psum.tile([P, PACK, P], F32, name="mm")
             cols = slice(s * P, s * P + P)
-            for t in range(PACK):
-                rows = slice(t * P, t * P + P)
+            for e in range(PACK):
+                rows = slice(e * P, e * P + P)
                 for g in range(NP):
                     nc.tensor.matmul_mx(
-                        out=bank[:, t, :],
-                        lhsT=kcodes[h][:, g, rows].bitcast(FP8X4),
-                        lhsT_scale=kscales[h][:, g, rows],
-                        rhs=vcodes[h][:, g, cols].bitcast(FP8X4),
-                        rhs_scale=vscales[h][:, g, cols],
+                        out=t[:, e, :],
+                        lhsT=made["kc", h][:, g, rows].bitcast(FP8X4),
+                        lhsT_scale=made["ks_", h][:, g, rows],
+                        rhs=made["vc", h][:, g, cols].bitcast(FP8X4),
+                        rhs_scale=made["vs_", h][:, g, cols],
                         start=(g == 0),
                         stop=(g == NP - 1),
                     )
-            nc.scalar.copy(out=vkg[h][:, cols, :], in_=bank[:].rearrange("p t d -> p d t"))
+            nc.scalar.copy(out=vkg[:, cols, :], in_=t[:].rearrange("p e d -> p d e"))
 
-        def quant_state(h, half):
-            cols = slice(256 * half, 256 * half + 256)
+        def quant_s(h, c):
+            codes = sbuf(("vkc", h), [P, DV], U32)
+            planes = sbuf(("vks", h), [P, DV], U8)
+            cols = slice(256 * c, 256 * c + 256)
             nc.vector.quantize_mx(
-                out=vkcodes[h][:, cols].bitcast(FP8X4),
-                scales=vkscales[h][:, cols],
-                in_=vkg[h][:, cols, :].rearrange("p d t -> p (d t)"),
+                out=codes[:, cols].bitcast(FP8X4),
+                scales=planes[:, cols],
+                in_=made["vkg", h][:, cols, :].rearrange("p d e -> p (d e)"),
             )
 
         def num(h, x):
             s, half = divmod(x, 2)
-            cols = slice(half * 512, half * 512 + 512)
-            bank = psum.tile([P, 512], F32, name="mm", bufs=4)
+            cols = slice(512 * half, 512 * half + 512)
+            t = psum.tile([P, 512], F32, name="mm")
             nc.tensor.matmul_mx(
-                out=bank[:],
-                lhsT=vkcodes[h][:, s * P : s * P + P].bitcast(FP8X4),
-                lhsT_scale=vkscales[h][:, s * P : s * P + P],
-                rhs=qcodes[h][:, cols].bitcast(FP8X4),
-                rhs_scale=qscales[h][:, cols],
+                out=t[:],
+                lhsT=made["vkc", h][:, s * P : s * P + P].bitcast(FP8X4),
+                lhsT_scale=made["vks", h][:, s * P : s * P + P],
+                rhs=made["qc", h][:, cols].bitcast(FP8X4),
+                rhs_scale=made["qs", h][:, cols],
                 start=True,
                 stop=True,
             )
-            num_ps[h, x] = bank
+            made["num", h, x] = t
 
         def mult(h, x):
             s, half = divmod(x, 2)
-            cols = slice(half * 512, half * 512 + 512)
-            if half == 0:
-                t_res = work.tile([P, N], F32, name="t_res", bufs=4)
-                res[h, s] = t_res
-            nc.vector.tensor_tensor(out=res[h, s][:, cols], in0=num_ps[h, x][:], in1=rb[h][:, cols], op=ALU.mult)
-            if half == 1:
-                nc.sync.dma_start(out=out_v[s, h // 2, h % 2], in_=res[h, s][:])
-
-        ctx.enter_context(tc.manual_schedule())
-
-        for h in range(H):
-            alloc_loads(h)
-        nc.scalar.dma_start(out=scol[:], in_=sc_v)
-        nc.sync.dma_start(out=raw_q[0][:, :, 0:256], in_=q_v[0][:, :, 0:256])
-        nc.sync.dma_start(out=raw_k[0][:, 0, :], in_=k_v[0][:, 0, :])
-        nc.sync.dma_start(out=raw_v[0][:, 0:2, :], in_=v_v[0][:, 0:2, :])
-        nc.sync.dma_start(out=raw_k[0][:, 1, :], in_=k_v[0][:, 1, :])
-        nc.sync.dma_start(out=raw_v[0][:, 2:4, :], in_=v_v[0][:, 2:4, :])
-        nc.sync.dma_start(out=raw_k[0][:, 2, :], in_=k_v[0][:, 2, :])
-        nc.sync.dma_start(out=raw_k[0][:, 3, :], in_=k_v[0][:, 3, :])
-        nc.sync.dma_start(out=raw_q[0][:, :, 256:1024], in_=q_v[0][:, :, 256:1024])
-        for h in range(1, H):
-            nc.sync.dma_start(out=raw_v[h][:], in_=v_v[h])
-            nc.sync.dma_start(out=raw_k[h][:], in_=k_v[h])
-            nc.sync.dma_start(out=raw_q[h][:], in_=q_v[h])
-
-        alloc_head(0)
-        relu_q(0, "v", 0, 256)
-        spread_scale()
-        for t in range(PACK):
-            relu_k(0, t)
-        split_ksum(0)
-        prod_v(0, 0)
-        prod_v(0, 1)
-        turn("k", 0, 0, 0)
-        turn("k", 0, 1, 0)
-        prod_v(0, 2)
-        prod_v(0, 3)
-        turn("v", 0, 0, 0)
-        turn("v", 0, 1, 0)
-        relu_q(0, "v", 256, 512)
-        turn("k", 0, 0, 1)
-        turn("k", 0, 1, 1)
-        turn("v", 0, 0, 1)
-        turn("v", 0, 1, 1)
-        relu_q(0, "v", 512, 1024)
-        quant_q(0, 0)
-        quant_k(0, 0)
-        quant_k(0, 1)
-        quant_q(0, 1)
-        den_mm(0, 0, 4)
-        quant_v(0, 0)
-        quant_v(0, 1)
-
-        for h in range(H):
-            n = h + 1
-            more = n < H
-            old = h - 1
-            if more:
-                alloc_head(n)
-                for t in range(PACK):
-                    relu_k(n, t)
-                split_ksum(n)
-            den_mm(h, 4, 8)
-            if old >= 0:
-                num(old, 4)
-                num(old, 5)
-            if more:
-                prod_v(n, 0)
-                prod_v(n, 1)
-            recip(h)
-            if old >= 0:
-                mult(old, 4)
-                mult(old, 5)
-            for s in range(PACK):
-                if s == 2 and old >= 0:
-                    num(old, 6)
-                    num(old, 7)
-                state(h, s)
-                if s == 1:
-                    if more:
-                        prod_v(n, 2)
-                    quant_state(h, 0)
-            if more:
-                prod_v(n, 3)
-            if old >= 0:
-                mult(old, 6)
-                mult(old, 7)
-            spread(h)
-            quant_state(h, 1)
-            if more:
-                relu_q(n, "v", 0, 512)
-                turn("v", n, 0, 0)
-                turn("v", n, 0, 1)
-                num(h, 0)
-                num(h, 1)
-                turn("v", n, 1, 0)
-                turn("v", n, 1, 1)
-                mult(h, 0)
-                mult(h, 1)
-                quant_v(n, 0)
-                quant_q(n, 0)
-                relu_q(n, "s", 512, 768)
-                turn("k", n, 0, 0)
-                turn("k", n, 0, 1)
-                quant_v(n, 1)
-                relu_q(n, "s", 768, 1024)
-                num(h, 2)
-                num(h, 3)
-                den_mm(n, 0, 4)
-                turn("k", n, 1, 0)
-                turn("k", n, 1, 1)
-                mult(h, 2)
-                quant_k(n, 0)
-                mult(h, 3)
-                quant_q(n, 1)
-                quant_k(n, 1)
+            cols = slice(512 * half, 512 * half + 512)
+            res = sbuf(("res", h, s), [P, N], F32, 4)
+            rb = made["rb", h]
+            if h == H - 1 and x in GPSIMD_MULT:
+                raw = sbuf(("raw", x), [P, 512], F32)
+                nc.scalar.copy(out=raw[:], in_=made["num", h, x][:])
+                nc.gpsimd.tensor_tensor(out=res[:, cols], in0=raw[:], in1=rb[:, cols], op=ALU.mult)
             else:
-                for x in range(8):
-                    num(h, x)
-                    mult(h, x)
+                nc.vector.tensor_tensor(out=res[:, cols], in0=made["num", h, x][:], in1=rb[:, cols], op=ALU.mult)
+            dst = out_v[s, h // 2, h % 2]
+            if h == H - 1 and s == PACK - 1:
+                nc.sync.dma_start(out=dst[:, cols], in_=res[:, cols])
+            elif half == 1:
+                nc.sync.dma_start(out=dst, in_=res[:])
+
+        steps = {
+            "scale": spread_scale,
+            "prod": prod,
+            "rq": relu_q,
+            "il": interleave,
+            "quant_q": quant_q,
+            "turn": turn,
+            "quant": quant,
+            "ks1": ks1,
+            "ks2": ks2,
+            "ks3": ks3,
+            "ks4": ks4,
+            "split": split,
+            "den": den,
+            "recip": recip,
+            "rt": row,
+            "state": state,
+            "quant_s": quant_s,
+            "num": num,
+            "mult": mult,
+        }
+        done = set()
+        for name, args in PROLOGUE:
+            steps[name](0, *args)
+            done.add((name, 0, args))
+        for period in range(-3, 8):
+            for name, lag, args in PERIOD:
+                h = period - lag
+                if 0 <= h < H and (name, h, args) not in done:
+                    steps[name](h, *args)
+                    done.add((name, h, args))

@@ -21,67 +21,68 @@ NP = N // PASS
 FLOPS = 2 * 2 * H * D * DV * N
 
 PROLOGUE = [
-    ('scale', ()),
-    ('prod', (2,)),
+    ('turn', ('k', 0, 0)),
+    ('wid', (0,)),
 ]
 PERIOD = [
-    ('den', 2, ()),
-    ('recip', 2, ()),
+    ('mult', 3, (0,)),
     ('il', 2, (0,)),
-    ('quant', 1, ('k', 0)),
-    ('state', 2, (0,)),
-    ('num', 3, (4,)),
+    ('den', 2, ()),
+    ('mult', 3, (1,)),
+    ('recip', 2, ()),
+    ('state', 3, (2,)),
+    ('quant', 2, ('v', 0)),
+    ('quant', 2, ('v', 1)),
+    ('turn', 1, ('k', 0, 1)),
     ('turn', 1, ('v', 0, 1)),
-    ('rt', 2, ()),
+    ('turn', 1, ('k', 1, 1)),
+    ('wid', 1, (0,)),
+    ('quant_s', 3, (1,)),
     ('turn', 1, ('v', 1, 1)),
     ('num', 3, (2,)),
-    ('state', 2, (1,)),
-    ('ks1', 1, ()),
-    ('mult', 3, (4,)),
-    ('prod', 1, (1,)),
-    ('rq', 1, (1,)),
-    ('mult', 3, (2,)),
-    ('il', 2, (3,)),
     ('num', 3, (3,)),
-    ('num', 3, (5,)),
-    ('quant_q', 2, (0,)),
-    ('il', 1, (2,)),
-    ('prod', 0, (3,)),
+    ('mult', 3, (2,)),
+    ('rt', 2, ()),
     ('mult', 3, (3,)),
-    ('state', 2, (2,)),
-    ('turn', 0, ('k', 1, 0)),
-    ('ks2', 1, ()),
+    ('num', 3, (4,)),
+    ('state', 2, (0,)),
     ('quant', 1, ('k', 1)),
-    ('turn', 1, ('v', 0, 0)),
-    ('ks3', 1, ()),
-    ('quant_s', 2, (0,)),
-    ('quant_q', 2, (1,)),
+    ('ks1', 1, ()),
+    ('il', 2, (3,)),
+    ('quant_q', 2, (0,)),
+    ('num', 3, (5,)),
+    ('il', 1, (2,)),
+    ('mult', 3, (4,)),
+    ('wid', 0, (1,)),
+    ('ks2', 1, ()),
+    ('wid', 0, (2,)),
+    ('state', 2, (1,)),
+    ('quant', 1, ('k', 0)),
     ('mult', 3, (5,)),
-    ('num', 3, (6,)),
-    ('rq', 0, (0,)),
+    ('ks3', 1, ()),
     ('state', 2, (3,)),
-    ('ks4', 1, ()),
-    ('num', 3, (7,)),
-    ('turn', 1, ('v', 1, 0)),
-    ('turn', 0, ('k', 0, 1)),
+    ('num', 3, (6,)),
+    ('quant_q', 2, (1,)),
     ('turn', 0, ('k', 0, 0)),
-    ('mult', 3, (6,)),
+    ('il', 1, (1,)),
+    ('ks4', 1, ()),
+    ('turn', 0, ('k', 1, 0)),
+    ('wid', 0, (3,)),
+    ('rq', 0, (0,)),
+    ('rq', 0, (1,)),
+    ('quant_s', 2, (0,)),
     ('split', 1, ()),
-    ('prod', 0, (2,)),
-    ('turn', 0, ('k', 1, 1)),
-    ('quant', 1, ('v', 0)),
+    ('mult', 3, (6,)),
+    ('turn', 1, ('v', 1, 0)),
+    ('turn', 1, ('v', 0, 0)),
+    ('num', 3, (7,)),
     ('num', 2, (0,)),
     ('num', 2, (1,)),
-    ('il', 1, (1,)),
     ('mult', 3, (7,)),
-    ('quant_s', 2, (1,)),
-    ('quant', 1, ('v', 1)),
-    ('prod', 0, (0,)),
-    ('mult', 2, (0,)),
-    ('mult', 2, (1,)),
 ]
-VECTOR_IL = {(0, 1), (1, 2), (3, 0)}
-GPSIMD_MULT = {4}
+VECTOR_IL = {(0, 1), (1, 3), (3, 3)}
+GPSIMD_MULT = {0}
+VECTOR_WIDEN = {(0, 0), (0, 1), (0, 2), (0, 3), (2, 1), (2, 2)}
 
 
 def tile_relu_linear_att_pa_kernel(tc, q, k, v_bytes, v_scale, out):
@@ -90,7 +91,7 @@ def tile_relu_linear_att_pa_kernel(tc, q, k, v_bytes, v_scale, out):
     v_v = v_bytes[0].rearrange("h (m s) n -> h m s n", s=PACK)
     q_v = q[0].rearrange("h (p j) n -> h p j n", j=PACK)
     out_v = out[0].rearrange("(m s a) (b n) -> s a b m n", s=PACK, a=2, b=2)
-    sc_v = v_scale[0, 0].rearrange("c (p i) -> (c p) i", i=N // P)
+    sc_v = v_scale[0, 0].rearrange("c (g p j) -> p (c g) j", g=NP, j=PACK)
 
     with ExitStack() as ctx:
         keep = ctx.enter_context(tc.tile_pool(name="keep", bufs=1))
@@ -110,8 +111,7 @@ def tile_relu_linear_att_pa_kernel(tc, q, k, v_bytes, v_scale, out):
         rden = keep.tile([P, 2, P], F32, name="rden")
         nc.gpsimd.memset(sel[:], 0.0)
         nc.gpsimd.memset(rden[:], 0.0)
-        scale = keep.tile([P, N], F32, name="scale", align_bytes=64)
-        scol = keep.tile([P, N // P], F32, name="scol")
+        scale = keep.tile([P, NP, PACK], F32, name="scale")
 
         ctx.enter_context(tc.manual_schedule())
 
@@ -127,7 +127,7 @@ def tile_relu_linear_att_pa_kernel(tc, q, k, v_bytes, v_scale, out):
             raw_k.append(t_k)
             raw_v.append(t_v)
             raw_q.append(t_q)
-        nc.scalar.dma_start(out=scol[:], in_=sc_v)
+        nc.scalar.dma_start(out=scale[:], in_=sc_v)
         for c in range(2):
             nc.sync.dma_start(out=raw_v[0][:, 2 * c : 2 * c + 2, :], in_=v_v[0][:, 2 * c : 2 * c + 2, :])
             nc.sync.dma_start(out=raw_k[0][:, 2 * c : 2 * c + 2, :], in_=k_v[0][:, 2 * c : 2 * c + 2, :])
@@ -152,19 +152,13 @@ def tile_relu_linear_att_pa_kernel(tc, q, k, v_bytes, v_scale, out):
                 made[key] = t
             return made[key]
 
-        def spread_scale(h):
-            for b in range(2):
-                t = psum.tile([P, 4, P], F32, name="tr")
-                for i in range(4):
-                    c = 4 * b + i
-                    nc.tensor.transpose(t[:, i, :], scol[:, c : c + 1].to_broadcast([P, P]), ident[:])
-                nc.vector.tensor_copy(
-                    out=scale[:].rearrange("m (p b i) -> m b p i", b=2, i=4)[:, b], in_=t[:].rearrange("m i p -> m p i")
-                )
-
-        def prod(h, s):
-            vp = sbuf(("vp", h), [P, PACK, N], BF16)
-            nc.vector.tensor_tensor(out=vp[:, s, :], in0=raw_v[h][:, s, :].bitcast(FP8), in1=scale[:], op=ALU.mult)
+        def widen(h, s):
+            wide = sbuf(("wide", h), [P, PACK, N], BF16)
+            src = raw_v[h][:, s, :].bitcast(FP8)
+            if (h, s) in VECTOR_WIDEN:
+                nc.vector.tensor_copy(out=wide[:, s, :], in_=src)
+            else:
+                nc.scalar.copy(out=wide[:, s, :], in_=src)
 
         def relu_q(h, c):
             rq = sbuf(("rq", h), [P, PACK, N], BF16)
@@ -192,23 +186,19 @@ def tile_relu_linear_att_pa_kernel(tc, q, k, v_bytes, v_scale, out):
             )
 
         def turn(h, kind, g, half):
-            words = (raw_k[h] if kind == "k" else made["vp", h])[:].bitcast(F32)
+            words = (raw_k[h] if kind == "k" else made["wide", h])[:].bitcast(F32)
             t = psum.tile([P, 2, 2, P], F32, name="tr")
             for u in range(2):
                 for r in range(2):
                     nc.tensor.transpose(t[:, u, r, :], words[:, 2 * half + r, 256 * g + u : 256 * (g + 1) : 2], ident[:])
             dst = sbuf(("grp", h, kind, g), [P, D, PACK], BF16, 6)[:, 256 * half : 256 * half + 256, :]
+            src = t[:].rearrange("p u r m -> p u (r m)").bitcast(BF16).rearrange("p u (c e) -> p c u e", e=2)
+            dst = dst.rearrange("p c (u e) -> p c u e", e=2)
             if kind == "k":
-                nc.scalar.activation(
-                    out=dst.rearrange("p c (u e) -> p c u e", e=2),
-                    in_=t[:].rearrange("p u r m -> p u (r m)").bitcast(BF16).rearrange("p u (c e) -> p c u e", e=2),
-                    func=ACT.Relu,
-                )
+                nc.scalar.activation(out=dst, in_=src, func=ACT.Relu)
             else:
-                nc.scalar.copy(
-                    out=dst.rearrange("p c j -> p (c j)").bitcast(F32).rearrange("p (c u) -> p c u", u=2),
-                    in_=t[:].rearrange("p u r m -> p (r m) u"),
-                )
+                factors = scale[:, g : g + 1, :].to_broadcast([P, 256, PACK]).rearrange("p c (u e) -> p c u e", e=2)
+                nc.vector.tensor_tensor(out=dst, in0=src, in1=factors, op=ALU.mult)
 
         def quant(h, kind, g):
             codes = sbuf((kind + "c", h), [P, NP, D], U32)
@@ -224,26 +214,31 @@ def tile_relu_linear_att_pa_kernel(tc, q, k, v_bytes, v_scale, out):
             for i in range(16):
                 for g in range(NP):
                     nc.tensor.matmul(
-                        t[:, i : i + 1],
+                        t[:, NP * i + g : NP * i + g + 1],
                         lhsT=made["grp", h, "k", g][:, 32 * i : 32 * i + 32, :].rearrange("p c j -> p (c j)"),
                         rhs=ones[:],
-                        start=(g == 0),
-                        stop=(g == NP - 1),
+                        start=True,
+                        stop=True,
                     )
 
         def ks2(h):
             part = sbuf(("part", h), [P, PACK, 4], F32)
-            nc.vector.tensor_copy(out=part[:], in_=made["ks", h][:, 0:16].rearrange("p (t b) -> p t b", b=4))
+            nc.vector.tensor_reduce(
+                out=part[:].rearrange("p t b -> p (t b)"),
+                in_=made["ks", h][:, 0:32].rearrange("p (i g) -> p i g", g=NP),
+                axis=AX.X,
+                op=ALU.add,
+            )
 
         def ks3(h):
             for b in range(4):
                 nc.tensor.matmul(
-                    made["ks", h][:, 16:20], lhsT=sel[:, b, :], rhs=made["part", h][:, :, b], start=(b == 0), stop=(b == 3)
+                    made["ks", h][:, 32:36], lhsT=sel[:, b, :], rhs=made["part", h][:, :, b], start=(b == 0), stop=(b == 3)
                 )
 
         def ks4(h):
             ksum = sbuf(("ksum", h), [P, PACK], F32)
-            nc.vector.tensor_copy(out=ksum[:], in_=made["ks", h][:, 16:20])
+            nc.vector.tensor_copy(out=ksum[:], in_=made["ks", h][:, 32:36])
 
         def split(h):
             ksum = made["ksum", h]
@@ -257,20 +252,20 @@ def tile_relu_linear_att_pa_kernel(tc, q, k, v_bytes, v_scale, out):
             nc.gpsimd.tensor_copy(out=parts[:, :, 2], in_=rest2[:])
 
         def den(h):
-            t = bank(("den", h), "tr", [P, N // P, 4])
+            t = bank(("den", h), "tr", [P, N // P, PACK, 4])
             for i in range(N // P):
                 for j in range(PACK):
                     nc.tensor.matmul(
-                        t[:, i, 0:3],
+                        t[:, i, j, 0:3],
                         lhsT=made["rq", h][:, j, i * P : i * P + P],
                         rhs=made["parts", h][:, j, 0:3],
-                        start=(j == 0),
-                        stop=(j == PACK - 1),
+                        start=True,
+                        stop=True,
                     )
 
         def recip(h):
             total = sbuf(("total", h), [P, N // P], F32)
-            nc.vector.tensor_reduce(out=total[:], in_=made["den", h][:, :, 0:3], axis=AX.X, op=ALU.add)
+            nc.vector.tensor_reduce(out=total[:], in_=made["den", h][:, :, :, 0:3], axis=AX.XY, op=ALU.add)
             nc.vector.reciprocal(out=rden[:, h % 2, 0 : N // P], in_=total[:])
 
         def row(h):
@@ -344,8 +339,7 @@ def tile_relu_linear_att_pa_kernel(tc, q, k, v_bytes, v_scale, out):
                 nc.sync.dma_start(out=dst, in_=res[:])
 
         steps = {
-            "scale": spread_scale,
-            "prod": prod,
+            "wid": widen,
             "rq": relu_q,
             "il": interleave,
             "quant_q": quant_q,

from contextlib import ExitStack

import concourse.mybir as mybir
from concourse.masks import make_identity

F32 = mybir.dt.float32
BF16 = mybir.dt.bfloat16
U32 = mybir.dt.uint32
U8 = mybir.dt.uint8
FP8 = mybir.dt.float8_e4m3fn
FP8X4 = mybir.dt.float8_e4m3fn_x4
ALU = mybir.AluOpType
ACT = mybir.ActivationFunctionType
AX = mybir.AxisListType

H, D, DV, N = 4, 512, 512, 1024
P = 128
PACK = 4
PASS = P * PACK
NP = N // PASS
FLOPS = 2 * 2 * H * D * DV * N

PROLOGUE = [
    ('turn', ('k', 0, 0)),
    ('wid', (0,)),
]
PERIOD = [
    ('mult', 3, (0,)),
    ('il', 2, (0,)),
    ('den', 2, ()),
    ('mult', 3, (1,)),
    ('recip', 2, ()),
    ('state', 3, (2,)),
    ('quant', 2, ('v', 0)),
    ('quant', 2, ('v', 1)),
    ('turn', 1, ('k', 0, 1)),
    ('turn', 1, ('v', 0, 1)),
    ('turn', 1, ('k', 1, 1)),
    ('wid', 1, (0,)),
    ('quant_s', 3, (1,)),
    ('turn', 1, ('v', 1, 1)),
    ('num', 3, (2,)),
    ('num', 3, (3,)),
    ('mult', 3, (2,)),
    ('rt', 2, ()),
    ('mult', 3, (3,)),
    ('num', 3, (4,)),
    ('state', 2, (0,)),
    ('quant', 1, ('k', 1)),
    ('ks1', 1, ()),
    ('il', 2, (3,)),
    ('quant_q', 2, (0,)),
    ('num', 3, (5,)),
    ('il', 1, (2,)),
    ('mult', 3, (4,)),
    ('wid', 0, (1,)),
    ('ks2', 1, ()),
    ('wid', 0, (2,)),
    ('state', 2, (1,)),
    ('quant', 1, ('k', 0)),
    ('mult', 3, (5,)),
    ('ks3', 1, ()),
    ('state', 2, (3,)),
    ('num', 3, (6,)),
    ('quant_q', 2, (1,)),
    ('turn', 0, ('k', 0, 0)),
    ('il', 1, (1,)),
    ('ks4', 1, ()),
    ('turn', 0, ('k', 1, 0)),
    ('wid', 0, (3,)),
    ('rq', 0, (0,)),
    ('rq', 0, (1,)),
    ('quant_s', 2, (0,)),
    ('split', 1, ()),
    ('mult', 3, (6,)),
    ('turn', 1, ('v', 1, 0)),
    ('turn', 1, ('v', 0, 0)),
    ('num', 3, (7,)),
    ('num', 2, (0,)),
    ('num', 2, (1,)),
    ('mult', 3, (7,)),
]
VECTOR_IL = {(0, 1), (1, 3), (3, 3)}
GPSIMD_MULT = {0}
VECTOR_WIDEN = {(0, 0), (0, 1), (0, 2), (0, 3), (2, 1), (2, 2)}


def tile_relu_linear_att_pa_kernel(tc, q, k, v_bytes, v_scale, out):
    nc = tc.nc
    k_v = k[0].rearrange("h (m t) n -> h m t n", t=PACK)
    v_v = v_bytes[0].rearrange("h (m s) n -> h m s n", s=PACK)
    q_v = q[0].rearrange("h (p j) n -> h p j n", j=PACK)
    out_v = out[0].rearrange("(m s a) (b n) -> s a b m n", s=PACK, a=2, b=2)
    sc_v = v_scale[0, 0].rearrange("c (g p j) -> p (c g) j", g=NP, j=PACK)

    with ExitStack() as ctx:
        keep = ctx.enter_context(tc.tile_pool(name="keep", bufs=1))
        ld = ctx.enter_context(tc.tile_pool(name="ld", bufs=4))
        work = ctx.enter_context(tc.tile_pool(name="work", bufs=2))
        psum = ctx.enter_context(tc.psum_pool(name="psum", bufs=4))

        ident = keep.tile([P, P], F32, name="ident")
        make_identity(nc, ident[:])
        warm = keep.tile([P, 1], F32, name="warm")
        nc.vector.memset(warm[:], 0.0)
        nc.scalar.activation(out=warm[:], in_=warm[:], func=ACT.Relu)
        ones = keep.tile([P, 1], BF16, name="ones")
        nc.vector.memset(ones[:], 1.0)
        quad = keep.tile([P, 32], F32, name="quad")
        sel = keep.tile([P, PACK, P], F32, name="sel")
        rden = keep.tile([P, 2, P], F32, name="rden")
        nc.gpsimd.memset(sel[:], 0.0)
        nc.gpsimd.memset(rden[:], 0.0)
        scale = keep.tile([P, NP, PACK], F32, name="scale")

        ctx.enter_context(tc.manual_schedule())

        nc.vector.tensor_reduce(out=quad[:], in_=ident[:].rearrange("p (c j) -> p c j", j=PACK), axis=AX.X, op=ALU.add)
        for b in range(PACK):
            nc.gpsimd.tensor_copy(out=sel[:, b, 32 * b : 32 * b + 32], in_=quad[:])

        raw_k, raw_v, raw_q = [], [], []
        for h in range(H):
            t_k = ld.tile([P, PACK, N], BF16, name="t_k")
            t_v = ld.tile([P, PACK, N], U8, name="t_v")
            t_q = ld.tile([P, PACK, N], BF16, name="t_q")
            raw_k.append(t_k)
            raw_v.append(t_v)
            raw_q.append(t_q)
        nc.scalar.dma_start(out=scale[:], in_=sc_v)
        for c in range(2):
            nc.sync.dma_start(out=raw_v[0][:, 2 * c : 2 * c + 2, :], in_=v_v[0][:, 2 * c : 2 * c + 2, :])
            nc.sync.dma_start(out=raw_k[0][:, 2 * c : 2 * c + 2, :], in_=k_v[0][:, 2 * c : 2 * c + 2, :])
        for c in range(2):
            nc.sync.dma_start(out=raw_q[0][:, :, 512 * c : 512 * c + 512], in_=q_v[0][:, :, 512 * c : 512 * c + 512])
        for h in range(1, H):
            nc.sync.dma_start(out=raw_k[h][:], in_=k_v[h])
            nc.sync.dma_start(out=raw_v[h][:], in_=v_v[h])
            nc.sync.dma_start(out=raw_q[h][:], in_=q_v[h])

        made = {}

        def sbuf(key, shape, dtype, bufs=2):
            if key not in made:
                t = work.tile(shape, dtype, name=key[0], align_bytes=64, bufs=bufs)
                made[key] = t
            return made[key]

        def bank(key, tag, shape):
            if key not in made:
                t = psum.tile(shape, F32, name=tag)
                made[key] = t
            return made[key]

        def widen(h, s):
            wide = sbuf(("wide", h), [P, PACK, N], BF16)
            src = raw_v[h][:, s, :].bitcast(FP8)
            if (h, s) in VECTOR_WIDEN:
                nc.vector.tensor_copy(out=wide[:, s, :], in_=src)
            else:
                nc.scalar.copy(out=wide[:, s, :], in_=src)

        def relu_q(h, c):
            rq = sbuf(("rq", h), [P, PACK, N], BF16)
            cols = slice(512 * c, 512 * c + 512)
            nc.vector.tensor_scalar(out=rq[:, :, cols], in0=raw_q[h][:, :, cols], scalar1=0.0, scalar2=None, op0=ALU.max)

        def interleave(h, c):
            qg = sbuf(("qg", h), [P, N, PACK], BF16)
            cols = slice(256 * c, 256 * c + 256)
            dst = qg[:, cols, :].rearrange("p (c i) j -> p c j i", i=4)
            src = made["rq", h][:, :, cols].rearrange("p j (c i) -> p c j i", i=4)
            if (h, c) in VECTOR_IL:
                nc.vector.tensor_copy(out=dst, in_=src)
            else:
                nc.scalar.copy(out=dst, in_=src)

        def quant_q(h, c):
            codes = sbuf(("qc", h), [P, N], U32, 3)
            planes = sbuf(("qs", h), [P, N], U8, 3)
            cols = slice(512 * c, 512 * c + 512)
            nc.vector.quantize_mx(
                out=codes[:, cols].bitcast(FP8X4),
                scales=planes[:, cols],
                in_=made["qg", h][:, cols, :].rearrange("p n j -> p (n j)"),
            )

        def turn(h, kind, g, half):
            words = (raw_k[h] if kind == "k" else made["wide", h])[:].bitcast(F32)
            t = psum.tile([P, 2, 2, P], F32, name="tr")
            for u in range(2):
                for r in range(2):
                    nc.tensor.transpose(t[:, u, r, :], words[:, 2 * half + r, 256 * g + u : 256 * (g + 1) : 2], ident[:])
            dst = sbuf(("grp", h, kind, g), [P, D, PACK], BF16, 6)[:, 256 * half : 256 * half + 256, :]
            src = t[:].rearrange("p u r m -> p u (r m)").bitcast(BF16).rearrange("p u (c e) -> p c u e", e=2)
            dst = dst.rearrange("p c (u e) -> p c u e", e=2)
            if kind == "k":
                nc.scalar.activation(out=dst, in_=src, func=ACT.Relu)
            else:
                factors = scale[:, g : g + 1, :].to_broadcast([P, 256, PACK]).rearrange("p c (u e) -> p c u e", e=2)
                nc.vector.tensor_tensor(out=dst, in0=src, in1=factors, op=ALU.mult)

        def quant(h, kind, g):
            codes = sbuf((kind + "c", h), [P, NP, D], U32)
            planes = sbuf((kind + "s_", h), [P, NP, D], U8)
            nc.vector.quantize_mx(
                out=codes[:, g, :].bitcast(FP8X4),
                scales=planes[:, g, :],
                in_=made["grp", h, kind, g][:].rearrange("p c j -> p (c j)"),
            )

        def ks1(h):
            t = bank(("ks", h), "tr", [P, PASS])
            for i in range(16):
                for g in range(NP):
                    nc.tensor.matmul(
                        t[:, NP * i + g : NP * i + g + 1],
                        lhsT=made["grp", h, "k", g][:, 32 * i : 32 * i + 32, :].rearrange("p c j -> p (c j)"),
                        rhs=ones[:],
                        start=True,
                        stop=True,
                    )

        def ks2(h):
            part = sbuf(("part", h), [P, PACK, 4], F32)
            nc.vector.tensor_reduce(
                out=part[:].rearrange("p t b -> p (t b)"),
                in_=made["ks", h][:, 0:32].rearrange("p (i g) -> p i g", g=NP),
                axis=AX.X,
                op=ALU.add,
            )

        def ks3(h):
            for b in range(4):
                nc.tensor.matmul(
                    made["ks", h][:, 32:36], lhsT=sel[:, b, :], rhs=made["part", h][:, :, b], start=(b == 0), stop=(b == 3)
                )

        def ks4(h):
            ksum = sbuf(("ksum", h), [P, PACK], F32)
            nc.vector.tensor_copy(out=ksum[:], in_=made["ks", h][:, 32:36])

        def split(h):
            ksum = made["ksum", h]
            parts = sbuf(("parts", h), [P, PACK, 4], BF16)
            rest1 = sbuf(("rest1", h), [P, PACK], F32)
            rest2 = sbuf(("rest2", h), [P, PACK], F32)
            nc.gpsimd.tensor_copy(out=parts[:, :, 0], in_=ksum[:])
            nc.gpsimd.tensor_tensor(out=rest1[:], in0=ksum[:], in1=parts[:, :, 0], op=ALU.subtract)
            nc.gpsimd.tensor_copy(out=parts[:, :, 1], in_=rest1[:])
            nc.gpsimd.tensor_tensor(out=rest2[:], in0=rest1[:], in1=parts[:, :, 1], op=ALU.subtract)
            nc.gpsimd.tensor_copy(out=parts[:, :, 2], in_=rest2[:])

        def den(h):
            t = bank(("den", h), "tr", [P, N // P, PACK, 4])
            for i in range(N // P):
                for j in range(PACK):
                    nc.tensor.matmul(
                        t[:, i, j, 0:3],
                        lhsT=made["rq", h][:, j, i * P : i * P + P],
                        rhs=made["parts", h][:, j, 0:3],
                        start=True,
                        stop=True,
                    )

        def recip(h):
            total = sbuf(("total", h), [P, N // P], F32)
            nc.vector.tensor_reduce(out=total[:], in_=made["den", h][:, :, :, 0:3], axis=AX.XY, op=ALU.add)
            nc.vector.reciprocal(out=rden[:, h % 2, 0 : N // P], in_=total[:])

        def row(h):
            t = bank(("row", h), "tr", [P, P])
            nc.tensor.transpose(t[:], rden[:, h % 2, :], ident[:])
            rrow = sbuf(("rrow", h), [32, P], F32)
            nc.scalar.copy(out=rrow[:], in_=t[0:32, :])
            park = out_v[PACK - 1, h // 2, h % 2][0:1, :]
            nc.sync.dma_start(out=park.rearrange("o (i p) -> (o i) p", p=P), in_=rrow[0 : N // P, :])
            rb = sbuf(("rb", h), [P, N], F32)
            nc.sync.dma_start(out=rb[:], in_=park.rearrange("o n -> (o n)").partition_broadcast(P))

        def state(h, s):
            vkg = sbuf(("vkg", h), [P, DV, PACK], BF16)
            t = psum.tile([P, PACK, P], F32, name="mm")
            cols = slice(s * P, s * P + P)
            for e in range(PACK):
                rows = slice(e * P, e * P + P)
                for g in range(NP):
                    nc.tensor.matmul_mx(
                        out=t[:, e, :],
                        lhsT=made["kc", h][:, g, rows].bitcast(FP8X4),
                        lhsT_scale=made["ks_", h][:, g, rows],
                        rhs=made["vc", h][:, g, cols].bitcast(FP8X4),
                        rhs_scale=made["vs_", h][:, g, cols],
                        start=(g == 0),
                        stop=(g == NP - 1),
                    )
            nc.scalar.copy(out=vkg[:, cols, :], in_=t[:].rearrange("p e d -> p d e"))

        def quant_s(h, c):
            codes = sbuf(("vkc", h), [P, DV], U32)
            planes = sbuf(("vks", h), [P, DV], U8)
            cols = slice(256 * c, 256 * c + 256)
            nc.vector.quantize_mx(
                out=codes[:, cols].bitcast(FP8X4),
                scales=planes[:, cols],
                in_=made["vkg", h][:, cols, :].rearrange("p d e -> p (d e)"),
            )

        def num(h, x):
            s, half = divmod(x, 2)
            cols = slice(512 * half, 512 * half + 512)
            t = psum.tile([P, 512], F32, name="mm")
            nc.tensor.matmul_mx(
                out=t[:],
                lhsT=made["vkc", h][:, s * P : s * P + P].bitcast(FP8X4),
                lhsT_scale=made["vks", h][:, s * P : s * P + P],
                rhs=made["qc", h][:, cols].bitcast(FP8X4),
                rhs_scale=made["qs", h][:, cols],
                start=True,
                stop=True,
            )
            made["num", h, x] = t

        def mult(h, x):
            s, half = divmod(x, 2)
            cols = slice(512 * half, 512 * half + 512)
            res = sbuf(("res", h, s), [P, N], F32, 4)
            rb = made["rb", h]
            if h == H - 1 and x in GPSIMD_MULT:
                raw = sbuf(("raw", x), [P, 512], F32)
                nc.scalar.copy(out=raw[:], in_=made["num", h, x][:])
                nc.gpsimd.tensor_tensor(out=res[:, cols], in0=raw[:], in1=rb[:, cols], op=ALU.mult)
            else:
                nc.vector.tensor_tensor(out=res[:, cols], in0=made["num", h, x][:], in1=rb[:, cols], op=ALU.mult)
            dst = out_v[s, h // 2, h % 2]
            if h == H - 1 and s == PACK - 1:
                nc.sync.dma_start(out=dst[:, cols], in_=res[:, cols])
            elif half == 1:
                nc.sync.dma_start(out=dst, in_=res[:])

        steps = {
            "wid": widen,
            "rq": relu_q,
            "il": interleave,
            "quant_q": quant_q,
            "turn": turn,
            "quant": quant,
            "ks1": ks1,
            "ks2": ks2,
            "ks3": ks3,
            "ks4": ks4,
            "split": split,
            "den": den,
            "recip": recip,
            "rt": row,
            "state": state,
            "quant_s": quant_s,
            "num": num,
            "mult": mult,
        }
        done = set()
        for name, args in PROLOGUE:
            steps[name](0, *args)
            done.add((name, 0, args))
        for period in range(-3, 8):
            for name, lag, args in PERIOD:
                h = period - lag
                if 0 <= h < H and (name, h, args) not in done:
                    steps[name](h, *args)
                    done.add((name, h, args))
